import numpy as np
import ml_dtypes


def mxq(x, axis, fmt="e4m3"):
    dtype, down = {"e4m3": (ml_dtypes.float8_e4m3fn, 7), "e5m2": (ml_dtypes.float8_e5m2, 14)}[fmt]
    v = np.moveaxis(np.asarray(x, np.float32).astype(ml_dtypes.bfloat16).astype(np.float64), axis, -1)
    blocks = v.reshape(v.shape[:-1] + (-1, 32))
    amax = np.abs(blocks).max(-1, keepdims=True)
    byte = np.maximum(np.where(amax > 0, np.frexp(amax)[1] - 1 + 127, 0) - down, 1)
    scale = np.exp2(byte - 127.0)
    codes = (blocks / scale).astype(np.float32).astype(dtype).astype(np.float64)
    return np.moveaxis((codes * scale).reshape(v.shape), -1, axis)


WIDE = False


def mx_kscale(k):
    if not WIDE:
        return np.ones(k)
    levels = np.array([10, -10, 5, -5, 0])
    a = np.random.permutation(np.resize(levels, k // 512 * 4)).reshape(k // 512, 4)
    idx = np.arange(k)
    return np.exp2(a[idx // 512, idx % 128 // 32])


BF16 = ml_dtypes.bfloat16


def bf(x):
    return np.asarray(x, np.float32).astype(BF16)


def f64(x):
    return np.asarray(x).astype(np.float64)


B, C, H, W, R, G, K = 1, 512, 32, 32, 512, 128, 7
PAD = K // 2
KK = K * K


def setup_inputs():
    t = mx_kscale(R)
    return {"x": bf(np.random.standard_normal((B, C, H, W))),
            "w_reduce": bf(np.random.standard_normal((R, C)) * 1.0 / np.sqrt(C) * t[:, None]),
            "b_reduce": bf(np.random.standard_normal(R) * 0.5 * t),
            "w_span": bf(np.random.standard_normal((KK * G, R)) * 1.5 / np.sqrt(R) / t[None, :]),
            "b_span": bf(np.random.standard_normal(KK * G) * 0.5)}


def reference(x, w_reduce, b_reduce, w_span, b_span):
    x = f64(x)
    red = np.maximum((mxq(f64(w_reduce), 1, "e4m3") @ mxq(x.reshape(B, C, H * W), 1, "e4m3")) + f64(b_reduce)[None, :, None], 0.0)
    kern = (mxq(f64(w_span), 1, "e4m3") @ mxq(red, 1, "e4m3")) + f64(b_span)[None, :, None]
    kern = kern.reshape(B, G, KK, H, W)
    e = np.exp(kern - kern.max(axis=2, keepdims=True))
    kern = e / e.sum(axis=2, keepdims=True)
    xp = np.pad(x, ((0, 0), (0, 0), (PAD, PAD), (PAD, PAD)))
    xg = xp.reshape(B, G, C // G, H + 2 * PAD, W + 2 * PAD)
    out = np.zeros((B, G, C // G, H, W))
    for i in range(K):
        for j in range(K):
            out = out + kern[:, :, None, i * K + j] * xg[:, :, :, i:i + H, j:j + W]
    return out.reshape(B, C, H, W)

@@ -1,0 +1,260 @@
+from contextlib import ExitStack
+
+import concourse.bass as bass
+import concourse.mybir as mybir
+import concourse.tile as tile
+from concourse.masks import make_identity
+
+F32 = mybir.dt.float32
+BF16 = mybir.dt.bfloat16
+U32 = mybir.dt.uint32
+U8 = mybir.dt.uint8
+FP8X4 = mybir.dt.float8_e4m3fn_x4
+ALU = mybir.AluOpType
+ACT = mybir.ActivationFunctionType
+
+P = 128
+CC = 4
+H = 32
+W = 32
+HW = H * W
+K7 = 7
+KK = K7 * K7
+PAD = 3
+HP = H + 2 * PAD
+WP = W + 2 * PAD
+R = 512
+NCH = 2
+CHR = H // NCH
+CHQ = CHR * W
+QB = CHQ // P
+WS_TAPS = 7
+FLOPS = 2 * 512 * 512 * HW + 2 * KK * P * R * HW + 2 * KK * 512 * HW
+
+
+def tile_involution_kernel(tc, x, w_reduce, b_reduce, w_span, b_span, out):
+    nc = tc.nc
+    with ExitStack() as ctx:
+        const = ctx.enter_context(tc.tile_pool(name="const", bufs=1))
+        wsp = ctx.enter_context(tc.tile_pool(name="wsp", bufs=4))
+        stage = ctx.enter_context(tc.tile_pool(name="stage", bufs=3))
+        psum = ctx.enter_context(tc.psum_pool(name="psum", bufs=3))
+        pacc = ctx.enter_context(tc.psum_pool(name="pacc", bufs=1))
+
+        x_sb = const.tile([P, CC * HW], BF16)
+        nc.sync.dma_start(out=x_sb[:], in_=x[0].rearrange("(g j) h w -> g (j h w)", j=CC))
+        wr_sb = const.tile([P, 4 * 512], BF16)
+        nc.sync.dma_start(
+            out=wr_sb[:].rearrange("p (u f) -> p u f", u=2),
+            in_=w_reduce.rearrange("(u p e) c -> p u (e c)", u=2, e=2),
+        )
+        br_b = const.tile([P, 4], BF16)
+        bs_b = const.tile([P, KK], BF16)
+        with nc.allow_non_contiguous_dma(reason="two small bias vectors"):
+            nc.sync.dma_start(
+                out=br_b[:].rearrange("p (u e) -> p u e", u=2),
+                in_=b_reduce.rearrange("(u p e) -> p u e", u=2, e=2),
+            )
+            nc.sync.dma_start(out=bs_b[:], in_=b_span.rearrange("(g t) -> g t", t=KK))
+        ws_view = w_span.rearrange("(g t) r -> g t r", t=KK)
+        ws_tiles = []
+
+        def load_ws(a):
+            ws_sb = wsp.tile([P, WS_TAPS * R], BF16, name="ws_sb")
+            nc.sync.dma_start(
+                out=ws_sb[:].rearrange("p (t r) -> p t r", t=WS_TAPS),
+                in_=ws_view[:, a * WS_TAPS : (a + 1) * WS_TAPS, :],
+            )
+            ws_tiles.append(ws_sb)
+
+        for a in range(4):
+            load_ws(a)
+
+        ident = const.tile([P, P], F32)
+        make_identity(nc, ident[:])
+
+        br = const.tile([P, 4], F32)
+        nc.vector.tensor_copy(out=br[:], in_=br_b[:])
+        bs = const.tile([P, KK], F32)
+        nc.vector.tensor_copy(out=bs[:], in_=bs_b[:])
+
+        xpad = const.tile([P, CC * HP * WP], BF16)
+        nc.gpsimd.memset(xpad[:], 0.0)
+        xpad4 = xpad[:].rearrange("p (j h w) -> p j h w", j=CC, w=WP)
+        nc.gpsimd.tensor_copy(
+            out=xpad4[:, :, PAD : PAD + H, PAD : PAD + W],
+            in_=x_sb[:].rearrange("p (j h w) -> p j h w", j=CC, w=W),
+        )
+
+        gx = const.tile([P, HW * 4], BF16, tag="grp", align_bytes=64)
+        nc.vector.tensor_copy(
+            out=gx[:].rearrange("p (q j) -> p q j", j=4),
+            in_=x_sb[:].rearrange("p (j q) -> p q j", j=4),
+        )
+        x_codes = const.tile([P, HW], U32, align_bytes=64)
+        x_scl = const.tile([P, HW], U8, align_bytes=64)
+        nc.vector.quantize_mx(out=x_codes[:].bitcast(FP8X4), scales=x_scl[:], in_=gx[:])
+
+        wr32 = wr_sb[:].bitcast(F32).rearrange("p (a w v) -> p a v w", a=4, v=2)
+        gw = const.tile([P, 4 * P * 4], BF16, align_bytes=64)
+        gw32 = gw[:].bitcast(F32).rearrange("p (a r v) -> p a r v", a=4, v=2)
+        for b in range(2):
+            tp = psum.tile([P, 512], F32, tag="mm", name="tp")
+            for a2 in range(2):
+                for v in range(2):
+                    nc.tensor.transpose(
+                        tp[:, (a2 * 2 + v) * P : (a2 * 2 + v + 1) * P], wr32[:, 2 * b + a2, v, :], ident[:]
+                    )
+            nc.scalar.copy(
+                out=gw32[:, 2 * b : 2 * b + 2, :, :],
+                in_=tp[:].rearrange("p (a v r) -> p a r v", a=2, v=2),
+            )
+        wr_codes = const.tile([P, 4 * P], U32, align_bytes=64)
+        wr_scl = const.tile([P, 4 * P], U8, align_bytes=64)
+        nc.vector.quantize_mx(out=wr_codes[:].bitcast(FP8X4), scales=wr_scl[:], in_=gw[:])
+
+        red_t = const.tile([P, 4 * HW], BF16)
+        for a in range(4):
+            for hf in range(2):
+                ps = psum.tile([P, 512], F32, tag="mm", name="ps")
+                nc.tensor.matmul_mx(
+                    out=ps[:],
+                    lhsT=wr_codes[:, a * P : (a + 1) * P].bitcast(FP8X4),
+                    lhsT_scale=wr_scl[:, a * P : (a + 1) * P],
+                    rhs=x_codes[:, hf * 512 : (hf + 1) * 512].bitcast(FP8X4),
+                    rhs_scale=x_scl[:, hf * 512 : (hf + 1) * 512],
+                    start=True,
+                    stop=True,
+                )
+                nc.scalar.activation(
+                    out=red_t[:, a * HW + hf * 512 : a * HW + (hf + 1) * 512],
+                    in_=ps[:],
+                    func=ACT.Relu,
+                    bias=br[:, a : a + 1],
+                    scale=1.0,
+                )
+        gr = const.tile([P, HW * 4], BF16, tag="grp", align_bytes=64)
+        nc.vector.tensor_copy(
+            out=gr[:].rearrange("p (q a) -> p q a", a=4),
+            in_=red_t[:].rearrange("p (a q) -> p q a", a=4),
+        )
+        red_codes = const.tile([P, HW], U32, align_bytes=64)
+        red_scl = const.tile([P, HW], U8, align_bytes=64)
+        nc.vector.quantize_mx(out=red_codes[:].bitcast(FP8X4), scales=red_scl[:], in_=gr[:])
+
+        ws_codes = const.tile([P, KK * P], U32, align_bytes=64)
+        ws_scl = const.tile([P, KK * P], U8, align_bytes=64)
+        for a in range(KK // WS_TAPS):
+            ws32 = ws_tiles[a][:].bitcast(F32).rearrange("p (t u w) -> p t u w", t=WS_TAPS, u=2)
+            t0 = 0
+            for n in (4, 2, 1):
+                gws = stage.tile([P, 4 * P * 4], BF16, name="gws", align_bytes=64)
+                gws32 = gws[:].bitcast(F32).rearrange("p (t g u) -> p t g u", t=4, u=2)
+                for b0 in range(0, n, 2):
+                    nb = min(2, n - b0)
+                    tp = psum.tile([P, 512], F32, tag="mm", name="tp")
+                    for tl in range(nb):
+                        for u in range(2):
+                            nc.tensor.transpose(
+                                tp[:, (tl * 2 + u) * P : (tl * 2 + u + 1) * P],
+                                ws32[:, t0 + b0 + tl, u, :],
+                                ident[:],
+                            )
+                    nc.scalar.copy(
+                        out=gws32[:, b0 : b0 + nb, :, :],
+                        in_=tp[:].rearrange("p (t u g) -> p t g u", t=2, u=2)[:, 0:nb, :, :],
+                    )
+                tg = a * WS_TAPS + t0
+                nc.vector.quantize_mx(
+                    out=ws_codes[:, tg * P : (tg + n) * P].bitcast(FP8X4),
+                    scales=ws_scl[:, tg * P : (tg + n) * P],
+                    in_=gws[:, 0 : n * P * 4],
+                )
+                t0 += n
+            if a + 4 < KK // WS_TAPS:
+                load_ws(a + 4)
+
+        def kern_pass(t, c):
+            ps = psum.tile([P, 512], F32, tag="mm", name="ps")
+            nc.tensor.matmul_mx(
+                out=ps[:],
+                lhsT=ws_codes[:, t * P : (t + 1) * P].bitcast(FP8X4),
+                lhsT_scale=ws_scl[:, t * P : (t + 1) * P],
+                rhs=red_codes[:, c * CHQ : (c + 1) * CHQ].bitcast(FP8X4),
+                rhs_scale=red_scl[:, c * CHQ : (c + 1) * CHQ],
+                start=True,
+                stop=True,
+            )
+            return ps
+
+        m = const.tile([P, HW], F32)
+        for t in range(KK):
+            for c in range(NCH):
+                ps = kern_pass(t, c)
+                mc = m[:, c * CHQ : (c + 1) * CHQ]
+                if t == 0:
+                    nc.vector.tensor_scalar_add(out=mc, in0=ps[:], scalar1=bs[:, 0:1])
+                else:
+                    nc.vector.scalar_tensor_tensor(
+                        out=mc, in0=ps[:], scalar=bs[:, t : t + 1], in1=mc, op0=ALU.add, op1=ALU.max
+                    )
+
+        out_v = out[0].rearrange("(g j) h w -> g j (h w)", j=CC)
+        for c in range(NCH):
+            acc = [pacc.tile([P, 512], F32, name="acc%d" % j) for j in range(CC)]
+            accz = pacc.tile([P, 512], F32, name="accz")
+            for t in range(KK):
+                ti = t // K7
+                tj = t % K7
+                ps = kern_pass(t, c)
+                d = stage.tile([P, CHQ], F32, name="d")
+                nc.vector.scalar_tensor_tensor(
+                    out=d[:],
+                    in0=ps[:],
+                    scalar=bs[:, t : t + 1],
+                    in1=m[:, c * CHQ : (c + 1) * CHQ],
+                    op0=ALU.add,
+                    op1=ALU.subtract,
+                )
+                e = stage.tile([P, CHQ], F32, name="e")
+                nc.scalar.activation(out=e[:], in_=d[:], func=ACT.Exp)
+                prod = stage.tile([P, CC * CHQ], F32, name="prod")
+                nc.vector.tensor_tensor(
+                    out=prod[:].rearrange("p (j h w) -> p j h w", j=CC, w=W),
+                    in0=e[:].rearrange("p (h w) -> p h w", w=W).unsqueeze(1).to_broadcast([P, CC, CHR, W]),
+                    in1=xpad4[:, :, c * CHR + ti : c * CHR + ti + CHR, tj : tj + W],
+                    op=ALU.mult,
+                )
+                for qb in range(QB):
+                    nc.tensor.matmul(
+                        out=accz[:, qb * P : (qb + 1) * P],
+                        lhsT=e[:, qb * P : (qb + 1) * P],
+                        rhs=ident[:],
+                        start=(t == 0 and qb == 0),
+                        stop=(t == KK - 1 and qb == QB - 1),
+                        is_transpose=True,
+                    )
+                for j in range(CC):
+                    for qb in range(QB):
+                        nc.tensor.matmul(
+                            out=acc[j][:, qb * P : (qb + 1) * P],
+                            lhsT=prod[:, j * CHQ + qb * P : j * CHQ + (qb + 1) * P],
+                            rhs=ident[:],
+                            start=(t == 0 and qb == 0),
+                            stop=(t == KK - 1 and qb == QB - 1),
+                            is_transpose=True,
+                        )
+            rz = stage.tile([P, 512], F32, name="rz")
+            nc.vector.reciprocal(out=rz[:], in_=accz[:])
+            osb = stage.tile([P, CC * CHQ], F32, name="osb", bufs=2)
+            for j in range(CC):
+                on = stage.tile([P, 512], F32, name="on")
+                nc.vector.tensor_tensor(out=on[:], in0=acc[j][:], in1=rz[:], op=ALU.mult)
+                pb = psum.tile([P, 512], F32, tag="mm", name="pb")
+                for qb in range(QB):
+                    nc.tensor.transpose(pb[:, qb * P : (qb + 1) * P], on[:, qb * P : (qb + 1) * P], ident[:])
+                nc.scalar.copy(out=osb[:, j * CHQ : (j + 1) * CHQ], in_=pb[:])
+            nc.sync.dma_start(
+                out=out_v[:, :, c * CHQ : (c + 1) * CHQ],
+                in_=osb[:].rearrange("p (j q) -> p j q", j=CC),
+            )

@@ -200,56 +200,69 @@ def tile_involution_kernel(tc, x, w_reduce, b_reduce, w_span, b_span, out):
                     )
 
         out_v = out[0].rearrange("(g j) h w -> g j (h w)", j=CC)
-        for c in range(NCH):
-            acc = [pacc.tile([P, 512], F32, name="acc%d" % j) for j in range(CC)]
-            accz = pacc.tile([P, 512], F32, name="accz")
-            for t in range(KK):
-                ti = t // K7
-                tj = t % K7
-                ps = kern_pass(t, c)
-                d = stage.tile([P, CHQ], F32, name="d")
-                nc.vector.scalar_tensor_tensor(
-                    out=d[:],
-                    in0=ps[:],
-                    scalar=bs[:, t : t + 1],
-                    in1=m[:, c * CHQ : (c + 1) * CHQ],
-                    op0=ALU.add,
-                    op1=ALU.subtract,
-                )
-                e = stage.tile([P, CHQ], F32, name="e")
-                nc.scalar.activation(out=e[:], in_=d[:], func=ACT.Exp)
-                prod = stage.tile([P, CC * CHQ], F32, name="prod")
-                nc.vector.tensor_tensor(
-                    out=prod[:].rearrange("p (j h w) -> p j h w", j=CC, w=W),
-                    in0=e[:].rearrange("p (h w) -> p h w", w=W).unsqueeze(1).to_broadcast([P, CC, CHR, W]),
-                    in1=xpad4[:, :, c * CHR + ti : c * CHR + ti + CHR, tj : tj + W],
-                    op=ALU.mult,
-                )
+        steps = [(c, t) for c in range(NCH) for t in range(KK)]
+        n_steps = len(steps)
+        ps_of = {}
+        e_of = {}
+        acc_of = {}
+
+        def stage_pass(s):
+            c, t = steps[s]
+            ps_of[s] = kern_pass(t, c)
+
+        def stage_exp(s):
+            c, t = steps[s]
+            d = stage.tile([P, CHQ], F32, name="d")
+            nc.vector.scalar_tensor_tensor(
+                out=d[:],
+                in0=ps_of[s][:],
+                scalar=bs[:, t : t + 1],
+                in1=m[:, c * CHQ : (c + 1) * CHQ],
+                op0=ALU.add,
+                op1=ALU.subtract,
+            )
+            e = stage.tile([P, CHQ], F32, name="e")
+            nc.scalar.activation(out=e[:], in_=d[:], func=ACT.Exp)
+            e_of[s] = e
+
+        def stage_sum(s):
+            c, t = steps[s]
+            ti = t // K7
+            tj = t % K7
+            if t == 0:
+                acc_of[c] = [pacc.tile([P, 512], F32, name="acc%d" % j) for j in range(CC + 1)]
+            acc = acc_of[c]
+            e = e_of[s]
+            prod = stage.tile([P, CC * CHQ], F32, name="prod")
+            nc.vector.tensor_tensor(
+                out=prod[:].rearrange("p (j h w) -> p j h w", j=CC, w=W),
+                in0=e[:].rearrange("p (h w) -> p h w", w=W).unsqueeze(1).to_broadcast([P, CC, CHR, W]),
+                in1=xpad4[:, :, c * CHR + ti : c * CHR + ti + CHR, tj : tj + W],
+                op=ALU.mult,
+            )
+            for j in [CC] + list(range(CC)):
                 for qb in range(QB):
+                    if j == CC:
+                        block = e[:, qb * P : (qb + 1) * P]
+                    else:
+                        block = prod[:, j * CHQ + qb * P : j * CHQ + (qb + 1) * P]
                     nc.tensor.matmul(
-                        out=accz[:, qb * P : (qb + 1) * P],
-                        lhsT=e[:, qb * P : (qb + 1) * P],
+                        out=acc[(j + 1) % (CC + 1)][:, qb * P : (qb + 1) * P],
+                        lhsT=block,
                         rhs=ident[:],
                         start=(t == 0 and qb == 0),
                         stop=(t == KK - 1 and qb == QB - 1),
                         is_transpose=True,
                     )
-                for j in range(CC):
-                    for qb in range(QB):
-                        nc.tensor.matmul(
-                            out=acc[j][:, qb * P : (qb + 1) * P],
-                            lhsT=prod[:, j * CHQ + qb * P : j * CHQ + (qb + 1) * P],
-                            rhs=ident[:],
-                            start=(t == 0 and qb == 0),
-                            stop=(t == KK - 1 and qb == QB - 1),
-                            is_transpose=True,
-                        )
+
+        def finish(c):
+            acc = acc_of[c]
             rz = stage.tile([P, 512], F32, name="rz")
-            nc.vector.reciprocal(out=rz[:], in_=accz[:])
+            nc.vector.reciprocal(out=rz[:], in_=acc[0][:])
             osb = stage.tile([P, CC * CHQ], F32, name="osb", bufs=2)
             for j in range(CC):
                 on = stage.tile([P, 512], F32, name="on")
-                nc.vector.tensor_tensor(out=on[:], in0=acc[j][:], in1=rz[:], op=ALU.mult)
+                nc.vector.tensor_tensor(out=on[:], in0=acc[j + 1][:], in1=rz[:], op=ALU.mult)
                 pb = psum.tile([P, 512], F32, tag="mm", name="pb")
                 for qb in range(QB):
                     nc.tensor.transpose(pb[:, qb * P : (qb + 1) * P], on[:, qb * P : (qb + 1) * P], ident[:])
@@ -258,3 +271,16 @@ def tile_involution_kernel(tc, x, w_reduce, b_reduce, w_span, b_span, out):
                 out=out_v[:, :, c * CHQ : (c + 1) * CHQ],
                 in_=osb[:].rearrange("p (j q) -> p j q", j=CC),
             )
+
+        with tc.manual_schedule():
+            stage_pass(0)
+            stage_pass(1)
+            stage_exp(0)
+            for s in range(n_steps):
+                if s + 2 < n_steps:
+                    stage_pass(s + 2)
+                if s + 1 < n_steps:
+                    stage_exp(s + 1)
+                stage_sum(s)
+                if steps[s][1] == KK - 1:
+                    finish(steps[s][0])

@@ -24,11 +24,14 @@ PAD = 3
 HP = H + 2 * PAD
 WP = W + 2 * PAD
 R = 512
-NCH = 2
+NCH = 4
 CHR = H // NCH
 CHQ = CHR * W
 QB = CHQ // P
 WS_TAPS = 7
+XK = W + PAD
+XL = 1352
+XWIN = CHR * XK
 FLOPS = 2 * 512 * 512 * HW + 2 * KK * P * R * HW + 2 * KK * 512 * HW
 
 
@@ -78,11 +81,15 @@ def tile_involution_kernel(tc, x, w_reduce, b_reduce, w_span, b_span, out):
         bs = const.tile([P, KK], F32)
         nc.vector.tensor_copy(out=bs[:], in_=bs_b[:])
 
-        xpad = const.tile([P, CC * HP * WP], BF16)
-        nc.gpsimd.memset(xpad[:], 0.0)
-        xpad4 = xpad[:].rearrange("p (j h w) -> p j h w", j=CC, w=WP)
+        ident_bf = const.tile([P, P], BF16)
+        make_identity(nc, ident_bf[:])
+        xp = const.tile([P, CC * XL], BF16)
+        nc.gpsimd.memset(xp[:], 0.0)
+        x0 = PAD + PAD * XK
         nc.gpsimd.tensor_copy(
-            out=xpad4[:, :, PAD : PAD + H, PAD : PAD + W],
+            out=xp[:]
+            .rearrange("p (j n) -> p j n", j=CC)[:, :, x0 : x0 + H * XK]
+            .rearrange("p j (h k) -> p j h k", k=XK)[:, :, :, 0:W],
             in_=x_sb[:].rearrange("p (j h w) -> p j h w", j=CC, w=W),
         )
 
@@ -174,24 +181,23 @@ def tile_involution_kernel(tc, x, w_reduce, b_reduce, w_span, b_span, out):
             if a + 4 < KK // WS_TAPS:
                 load_ws(a + 4)
 
-        def kern_pass(t, c):
-            ps = psum.tile([P, 512], F32, tag="mm", name="ps")
+        def kern_pass(dst, t, q0, nq):
             nc.tensor.matmul_mx(
-                out=ps[:],
+                out=dst,
                 lhsT=ws_codes[:, t * P : (t + 1) * P].bitcast(FP8X4),
                 lhsT_scale=ws_scl[:, t * P : (t + 1) * P],
-                rhs=red_codes[:, c * CHQ : (c + 1) * CHQ].bitcast(FP8X4),
-                rhs_scale=red_scl[:, c * CHQ : (c + 1) * CHQ],
+                rhs=red_codes[:, q0 : q0 + nq].bitcast(FP8X4),
+                rhs_scale=red_scl[:, q0 : q0 + nq],
                 start=True,
                 stop=True,
             )
-            return ps
 
         m = const.tile([P, HW], F32)
         for t in range(KK):
-            for c in range(NCH):
-                ps = kern_pass(t, c)
-                mc = m[:, c * CHQ : (c + 1) * CHQ]
+            for hf in range(2):
+                ps = psum.tile([P, 512], F32, tag="mm", name="ps")
+                kern_pass(ps[:], t, hf * 512, 512)
+                mc = m[:, hf * 512 : (hf + 1) * 512]
                 if t == 0:
                     nc.vector.tensor_scalar_add(out=mc, in0=ps[:], scalar1=bs[:, 0:1])
                 else:
@@ -200,87 +206,144 @@ def tile_involution_kernel(tc, x, w_reduce, b_reduce, w_span, b_span, out):
                     )
 
         out_v = out[0].rearrange("(g j) h w -> g j (h w)", j=CC)
-        steps = [(c, t) for c in range(NCH) for t in range(KK)]
-        n_steps = len(steps)
+        units = [(c, [t for t in (t0, t0 + 1) if t < KK]) for c in range(NCH) for t0 in range(0, KK, 2)]
+        n_units = len(units)
         ps_of = {}
         e_of = {}
         acc_of = {}
+        xw_of = {}
 
-        def stage_pass(s):
-            c, t = steps[s]
-            ps_of[s] = kern_pass(t, c)
+        def load_windows(c):
+            xw0 = pacc.tile([P, 1024], BF16, name="xw0")
+            xw1 = pacc.tile([P, 1024], BF16, name="xw1")
+            for dst, j in ((xw0[:, 0:512], 0), (xw0[:, 512:1024], 1), (xw1[:, 0:512], 2)):
+                nc.tensor.matmul(
+                    out=dst,
+                    lhsT=ident_bf[:],
+                    rhs=xp[:, j * XL + c * XWIN : j * XL + c * XWIN + 512],
+                    start=True,
+                    stop=True,
+                )
+            xw_of[c] = (xw0, xw1)
 
-        def stage_exp(s):
-            c, t = steps[s]
-            d = stage.tile([P, CHQ], F32, name="d")
-            nc.vector.scalar_tensor_tensor(
-                out=d[:],
-                in0=ps_of[s][:],
-                scalar=bs[:, t : t + 1],
-                in1=m[:, c * CHQ : (c + 1) * CHQ],
-                op0=ALU.add,
-                op1=ALU.subtract,
-            )
-            e = stage.tile([P, CHQ], F32, name="e")
-            nc.scalar.activation(out=e[:], in_=d[:], func=ACT.Exp)
-            e_of[s] = e
+        def stage_pass(u):
+            c, taps = units[u]
+            ps = psum.tile([P, 512], F32, tag="mm", name="ps")
+            for k, t in enumerate(taps):
+                kern_pass(ps[:, k * CHQ : (k + 1) * CHQ], t, c * CHQ, CHQ)
+            ps_of[u] = ps
 
-        def stage_sum(s):
-            c, t = steps[s]
-            ti = t // K7
-            tj = t % K7
-            if t == 0:
-                acc_of[c] = [pacc.tile([P, 512], F32, name="acc%d" % j) for j in range(CC + 1)]
-            acc = acc_of[c]
-            e = e_of[s]
-            prod = stage.tile([P, CC * CHQ], F32, name="prod")
+        def stage_exp(u):
+            c, taps = units[u]
+            n = len(taps)
+            d = stage.tile([P, 512], F32, name="d")
             nc.vector.tensor_tensor(
-                out=prod[:].rearrange("p (j h w) -> p j h w", j=CC, w=W),
-                in0=e[:].rearrange("p (h w) -> p h w", w=W).unsqueeze(1).to_broadcast([P, CC, CHR, W]),
-                in1=xpad4[:, :, c * CHR + ti : c * CHR + ti + CHR, tj : tj + W],
-                op=ALU.mult,
+                out=d[:, 0 : n * CHQ].rearrange("p (k q) -> p k q", k=n),
+                in0=ps_of[u][:, 0 : n * CHQ].rearrange("p (k q) -> p k q", k=n),
+                in1=m[:, c * CHQ : (c + 1) * CHQ].unsqueeze(1).to_broadcast([P, n, CHQ]),
+                op=ALU.subtract,
             )
-            for j in [CC] + list(range(CC)):
+            e = stage.tile([P, 512], F32, name="e")
+            for k, t in enumerate(taps):
+                nc.scalar.activation(
+                    out=e[:, k * CHQ : (k + 1) * CHQ],
+                    in_=d[:, k * CHQ : (k + 1) * CHQ],
+                    func=ACT.Exp,
+                    bias=bs[:, t : t + 1],
+                    scale=1.0,
+                )
+            e_of[u] = e
+
+        def add_block(bank, slot, block, first, last):
+            nc.tensor.matmul(
+                out=bank[:, slot * P : (slot + 1) * P],
+                lhsT=block,
+                rhs=ident[:],
+                start=first,
+                stop=last,
+                is_transpose=True,
+            )
+
+        def stage_sum(u):
+            c, taps = units[u]
+            if taps[0] == 0:
+                acc_of[c] = [pacc.tile([P, 512], F32, name="acc%d" % i) for i in range(3)]
+            accz, acc_a, acc_b = acc_of[c]
+            xw0, xw1 = xw_of[c]
+            e = e_of[u]
+            for k, t in enumerate(taps):
+                off = (t // K7) * XK + t % K7
+                ek = e[:, k * CHQ : (k + 1) * CHQ]
+                ek3 = ek.rearrange("p (h w) -> p h w", w=W)
+                pg = stage.tile([P, CHQ], F32, name="pg", bufs=6)
+                g0 = 3 * XL + c * XWIN + off
+                nc.gpsimd.tensor_tensor(
+                    out=pg[:].rearrange("p (h w) -> p h w", w=W),
+                    in0=ek3,
+                    in1=xp[:, g0 : g0 + XWIN].rearrange("p (h k) -> p h k", k=XK)[:, :, 0:W],
+                    op=ALU.mult,
+                )
+                pv = stage.tile([P, 3 * CHQ], F32, name="pv", bufs=6)
+                nc.vector.tensor_tensor(
+                    out=pv[:, 0 : 2 * CHQ].rearrange("p (j h w) -> p j h w", j=2, w=W),
+                    in0=xw0[:]
+                    .rearrange("p (j n) -> p j n", j=2)[:, :, off : off + XWIN]
+                    .rearrange("p j (h k) -> p j h k", k=XK)[:, :, :, 0:W],
+                    in1=ek3.unsqueeze(1).to_broadcast([P, 2, CHR, W]),
+                    op=ALU.mult,
+                )
+                nc.vector.tensor_tensor(
+                    out=pv[:, 2 * CHQ : 3 * CHQ].rearrange("p (h w) -> p h w", w=W),
+                    in0=xw1[:, off : off + XWIN].rearrange("p (h k) -> p h k", k=XK)[:, :, 0:W],
+                    in1=ek3,
+                    op=ALU.mult,
+                )
+                first = t == 0
+                last = t == KK - 1
                 for qb in range(QB):
-                    if j == CC:
-                        block = e[:, qb * P : (qb + 1) * P]
-                    else:
-                        block = prod[:, j * CHQ + qb * P : j * CHQ + (qb + 1) * P]
-                    nc.tensor.matmul(
-                        out=acc[(j + 1) % (CC + 1)][:, qb * P : (qb + 1) * P],
-                        lhsT=block,
-                        rhs=ident[:],
-                        start=(t == 0 and qb == 0),
-                        stop=(t == KK - 1 and qb == QB - 1),
-                        is_transpose=True,
-                    )
+                    add_block(accz, qb, ek[:, qb * P : (qb + 1) * P], first and qb == 0, last and qb == QB - 1)
+                for i in range(2 * QB):
+                    add_block(acc_a, i, pv[:, i * P : (i + 1) * P], first and i == 0, last and i == 2 * QB - 1)
+                for qb in range(QB):
+                    add_block(acc_b, qb, pv[:, (2 * QB + qb) * P : (2 * QB + qb + 1) * P], first and qb == 0, False)
+                for qb in range(QB):
+                    add_block(acc_b, QB + qb, pg[:, qb * P : (qb + 1) * P], False, last and qb == QB - 1)
 
         def finish(c):
-            acc = acc_of[c]
-            rz = stage.tile([P, 512], F32, name="rz")
-            nc.vector.reciprocal(out=rz[:], in_=acc[0][:])
+            accz, acc_a, acc_b = acc_of[c]
+            rz = stage.tile([P, CHQ], F32, name="rz")
+            nc.vector.reciprocal(out=rz[:], in_=accz[:, 0:CHQ])
             osb = stage.tile([P, CC * CHQ], F32, name="osb", bufs=2)
-            for j in range(CC):
+            for i, bank in enumerate((acc_a, acc_b)):
                 on = stage.tile([P, 512], F32, name="on")
-                nc.vector.tensor_tensor(out=on[:], in0=acc[j + 1][:], in1=rz[:], op=ALU.mult)
+                nc.vector.tensor_tensor(
+                    out=on[:].rearrange("p (j n) -> p j n", j=2),
+                    in0=bank[:].rearrange("p (j n) -> p j n", j=2),
+                    in1=rz[:].unsqueeze(1).to_broadcast([P, 2, CHQ]),
+                    op=ALU.mult,
+                )
                 pb = psum.tile([P, 512], F32, tag="mm", name="pb")
-                for qb in range(QB):
-                    nc.tensor.transpose(pb[:, qb * P : (qb + 1) * P], on[:, qb * P : (qb + 1) * P], ident[:])
-                nc.scalar.copy(out=osb[:, j * CHQ : (j + 1) * CHQ], in_=pb[:])
+                for s in range(4):
+                    nc.tensor.transpose(pb[:, s * P : (s + 1) * P], on[:, s * P : (s + 1) * P], ident[:])
+                nc.scalar.copy(out=osb[:, i * 512 : (i + 1) * 512], in_=pb[:])
             nc.sync.dma_start(
                 out=out_v[:, :, c * CHQ : (c + 1) * CHQ],
                 in_=osb[:].rearrange("p (j q) -> p j q", j=CC),
             )
 
         with tc.manual_schedule():
+            load_windows(0)
             stage_pass(0)
             stage_pass(1)
             stage_exp(0)
-            for s in range(n_steps):
-                if s + 2 < n_steps:
-                    stage_pass(s + 2)
-                if s + 1 < n_steps:
-                    stage_exp(s + 1)
-                stage_sum(s)
-                if steps[s][1] == KK - 1:
-                    finish(steps[s][0])
+            for u in range(n_units):
+                if u + 2 < n_units:
+                    stage_pass(u + 2)
+                if u + 1 < n_units:
+                    stage_exp(u + 1)
+                stage_sum(u)
+                c, taps = units[u]
+                if taps[-1] == KK - 1:
+                    finish(c)
+                    if c + 1 < NCH:
+                        load_windows(c + 1)

@@ -39,7 +39,7 @@ def tile_involution_kernel(tc, x, w_reduce, b_reduce, w_span, b_span, out):
     nc = tc.nc
     with ExitStack() as ctx:
         const = ctx.enter_context(tc.tile_pool(name="const", bufs=1))
-        wsp = ctx.enter_context(tc.tile_pool(name="wsp", bufs=4))
+        wsp = ctx.enter_context(tc.tile_pool(name="wsp", bufs=3))
         stage = ctx.enter_context(tc.tile_pool(name="stage", bufs=3))
         psum = ctx.enter_context(tc.psum_pool(name="psum", bufs=3))
         pacc = ctx.enter_context(tc.psum_pool(name="pacc", bufs=1))
@@ -70,7 +70,7 @@ def tile_involution_kernel(tc, x, w_reduce, b_reduce, w_span, b_span, out):
             )
             ws_tiles.append(ws_sb)
 
-        for a in range(4):
+        for a in range(3):
             load_ws(a)
 
         ident = const.tile([P, P], F32)
@@ -106,7 +106,7 @@ def tile_involution_kernel(tc, x, w_reduce, b_reduce, w_span, b_span, out):
         gw = const.tile([P, 4 * P * 4], BF16, align_bytes=64)
         gw32 = gw[:].bitcast(F32).rearrange("p (a r v) -> p a r v", a=4, v=2)
         for b in range(2):
-            tp = psum.tile([P, 512], F32, tag="mm", name="tp")
+            tp = pacc.tile([P, 512], F32, tag="acc%d" % b, name="tp")
             for a2 in range(2):
                 for v in range(2):
                     nc.tensor.transpose(
@@ -151,7 +151,9 @@ def tile_involution_kernel(tc, x, w_reduce, b_reduce, w_span, b_span, out):
 
         ws_codes = const.tile([P, KK * P], U32, align_bytes=64)
         ws_scl = const.tile([P, KK * P], U8, align_bytes=64)
-        for a in range(KK // WS_TAPS):
+        n_banks = [0]
+
+        def prepare_ws(a):
             ws32 = ws_tiles[a][:].bitcast(F32).rearrange("p (t u w) -> p t u w", t=WS_TAPS, u=2)
             t0 = 0
             for n in (4, 2, 1):
@@ -159,7 +161,8 @@ def tile_involution_kernel(tc, x, w_reduce, b_reduce, w_span, b_span, out):
                 gws32 = gws[:].bitcast(F32).rearrange("p (t g u) -> p t g u", t=4, u=2)
                 for b0 in range(0, n, 2):
                     nb = min(2, n - b0)
-                    tp = psum.tile([P, 512], F32, tag="mm", name="tp")
+                    tp = pacc.tile([P, 512], F32, tag="acc%d" % (n_banks[0] % 3), name="tp")
+                    n_banks[0] += 1
                     for tl in range(nb):
                         for u in range(2):
                             nc.tensor.transpose(
@@ -178,81 +181,140 @@ def tile_involution_kernel(tc, x, w_reduce, b_reduce, w_span, b_span, out):
                     in_=gws[:, 0 : n * P * 4],
                 )
                 t0 += n
-            if a + 4 < KK // WS_TAPS:
-                load_ws(a + 4)
-
-        def kern_pass(dst, t, q0, nq):
-            nc.tensor.matmul_mx(
-                out=dst,
-                lhsT=ws_codes[:, t * P : (t + 1) * P].bitcast(FP8X4),
-                lhsT_scale=ws_scl[:, t * P : (t + 1) * P],
-                rhs=red_codes[:, q0 : q0 + nq].bitcast(FP8X4),
-                rhs_scale=red_scl[:, q0 : q0 + nq],
-                start=True,
-                stop=True,
-            )
-
-        m = const.tile([P, HW], F32)
-        for t in range(KK):
-            for hf in range(2):
-                ps = psum.tile([P, 512], F32, tag="mm", name="ps")
-                kern_pass(ps[:], t, hf * 512, 512)
-                mc = m[:, hf * 512 : (hf + 1) * 512]
-                if t == 0:
-                    nc.vector.tensor_scalar_add(out=mc, in0=ps[:], scalar1=bs[:, 0:1])
-                else:
-                    nc.vector.scalar_tensor_tensor(
-                        out=mc, in0=ps[:], scalar=bs[:, t : t + 1], in1=mc, op0=ALU.add, op1=ALU.max
-                    )
+            if a + 3 < KK // WS_TAPS:
+                load_ws(a + 3)
 
         out_v = out[0].rearrange("(g j) h w -> g j (h w)", j=CC)
         units = [(c, [t for t in (t0, t0 + 1) if t < KK]) for c in range(NCH) for t0 in range(0, KK, 2)]
         n_units = len(units)
+        upc = n_units // NCH
+        LEAD = upc + 2
         ps_of = {}
+        kb_of = {}
         e_of = {}
+        pr_of = {}
         acc_of = {}
         xw_of = {}
+        mm_of = {}
+        ms_of = {}
+        mp_of = {}
 
         def load_windows(c):
             xw0 = pacc.tile([P, 1024], BF16, name="xw0")
-            xw1 = pacc.tile([P, 1024], BF16, name="xw1")
-            for dst, j in ((xw0[:, 0:512], 0), (xw0[:, 512:1024], 1), (xw1[:, 0:512], 2)):
+            for j in range(2):
                 nc.tensor.matmul(
-                    out=dst,
+                    out=xw0[:, j * 512 : (j + 1) * 512],
                     lhsT=ident_bf[:],
                     rhs=xp[:, j * XL + c * XWIN : j * XL + c * XWIN + 512],
                     start=True,
                     stop=True,
                 )
-            xw_of[c] = (xw0, xw1)
+            xw_of[c] = xw0
 
         def stage_pass(u):
             c, taps = units[u]
             ps = psum.tile([P, 512], F32, tag="mm", name="ps")
             for k, t in enumerate(taps):
-                kern_pass(ps[:, k * CHQ : (k + 1) * CHQ], t, c * CHQ, CHQ)
+                nc.tensor.matmul_mx(
+                    out=ps[:, k * CHQ : (k + 1) * CHQ],
+                    lhsT=ws_codes[:, t * P : (t + 1) * P].bitcast(FP8X4),
+                    lhsT_scale=ws_scl[:, t * P : (t + 1) * P],
+                    rhs=red_codes[:, c * CHQ : (c + 1) * CHQ].bitcast(FP8X4),
+                    rhs_scale=red_scl[:, c * CHQ : (c + 1) * CHQ],
+                    start=True,
+                    stop=True,
+                )
             ps_of[u] = ps
+
+        def stage_max(u, k):
+            c, taps = units[u]
+            if k >= len(taps):
+                return
+            t = taps[k]
+            if t == 0:
+                mm_of[c] = stage.tile([P, 512], F32, name="mm", bufs=2)
+            mk = mm_of[c][:, k * CHQ : (k + 1) * CHQ]
+            pk = ps_of[u][:, k * CHQ : (k + 1) * CHQ]
+            if t < 2:
+                nc.vector.tensor_scalar_add(out=mk, in0=pk, scalar1=bs[:, t : t + 1])
+            else:
+                nc.vector.scalar_tensor_tensor(
+                    out=mk, in0=pk, scalar=bs[:, t : t + 1], in1=mk, op0=ALU.add, op1=ALU.max
+                )
+
+        def stage_copy(u):
+            n = len(units[u][1]) * CHQ
+            kb = stage.tile([P, 512], F32, name="kb", bufs=LEAD + 2)
+            nc.scalar.copy(out=kb[:, 0:n], in_=ps_of[u][:, 0:n])
+            kb_of[u] = kb
+
+        def merge_max(c):
+            ms = stage.tile([P, CHQ], F32, name="ms", bufs=2)
+            nc.vector.tensor_tensor(out=ms[:], in0=mm_of[c][:, 0:CHQ], in1=mm_of[c][:, CHQ : 2 * CHQ], op=ALU.max)
+            ms_of[c] = ms
+
+        def max_to_psum(c):
+            mp = pacc.tile([P, CHQ], F32, name="mp")
+            nc.tensor.matmul(out=mp[:], lhsT=ident[:], rhs=ms_of[c][:], start=True, stop=True)
+            mp_of[c] = mp
+
+        def stage_sub(u):
+            c, taps = units[u]
+            n = len(taps)
+            kb3 = kb_of[u][:, 0 : n * CHQ].rearrange("p (k q) -> p k q", k=n)
+            nc.vector.tensor_tensor(
+                out=kb3,
+                in0=kb3,
+                in1=mp_of[c][:].unsqueeze(1).to_broadcast([P, n, CHQ]),
+                op=ALU.subtract,
+            )
 
         def stage_exp(u):
             c, taps = units[u]
-            n = len(taps)
-            d = stage.tile([P, 512], F32, name="d")
-            nc.vector.tensor_tensor(
-                out=d[:, 0 : n * CHQ].rearrange("p (k q) -> p k q", k=n),
-                in0=ps_of[u][:, 0 : n * CHQ].rearrange("p (k q) -> p k q", k=n),
-                in1=m[:, c * CHQ : (c + 1) * CHQ].unsqueeze(1).to_broadcast([P, n, CHQ]),
-                op=ALU.subtract,
-            )
-            e = stage.tile([P, 512], F32, name="e")
+            e = stage.tile([P, 512], F32, name="e", bufs=4)
             for k, t in enumerate(taps):
                 nc.scalar.activation(
                     out=e[:, k * CHQ : (k + 1) * CHQ],
-                    in_=d[:, k * CHQ : (k + 1) * CHQ],
+                    in_=kb_of[u][:, k * CHQ : (k + 1) * CHQ],
                     func=ACT.Exp,
                     bias=bs[:, t : t + 1],
                     scale=1.0,
                 )
             e_of[u] = e
+            pr_of[u] = []
+
+        def stage_product(u, k):
+            c, taps = units[u]
+            if k >= len(taps):
+                return
+            t = taps[k]
+            off = (t // K7) * XK + t % K7
+            ek4 = (
+                e_of[u][:, k * CHQ : (k + 1) * CHQ]
+                .rearrange("p (h w) -> p h w", w=W)
+                .unsqueeze(1)
+                .to_broadcast([P, 2, CHR, W])
+            )
+            pg = stage.tile([P, 2 * CHQ], F32, name="pg", bufs=5)
+            g0 = c * XWIN + off
+            nc.gpsimd.tensor_tensor(
+                out=pg[:].rearrange("p (j h w) -> p j h w", j=2, w=W),
+                in0=ek4,
+                in1=xp[:]
+                .rearrange("p (j n) -> p j n", j=CC)[:, 2:4, g0 : g0 + XWIN]
+                .rearrange("p j (h k) -> p j h k", k=XK)[:, :, :, 0:W],
+                op=ALU.mult,
+            )
+            pv = stage.tile([P, 2 * CHQ], F32, name="pv", bufs=5)
+            nc.vector.tensor_tensor(
+                out=pv[:].rearrange("p (j h w) -> p j h w", j=2, w=W),
+                in0=xw_of[c][:]
+                .rearrange("p (j n) -> p j n", j=2)[:, :, off : off + XWIN]
+                .rearrange("p j (h k) -> p j h k", k=XK)[:, :, :, 0:W],
+                in1=ek4,
+                op=ALU.mult,
+            )
+            pr_of[u].append((pv, pg))
 
         def add_block(bank, slot, block, first, last):
             nc.tensor.matmul(
@@ -264,64 +326,41 @@ def tile_involution_kernel(tc, x, w_reduce, b_reduce, w_span, b_span, out):
                 is_transpose=True,
             )
 
-        def stage_sum(u):
+        def stage_add(u):
             c, taps = units[u]
             if taps[0] == 0:
-                acc_of[c] = [pacc.tile([P, 512], F32, name="acc%d" % i) for i in range(3)]
+                acc_of[c] = [pacc.tile([P, 512], F32, tag="acc%d" % i, name="acc") for i in range(3)]
             accz, acc_a, acc_b = acc_of[c]
-            xw0, xw1 = xw_of[c]
-            e = e_of[u]
             for k, t in enumerate(taps):
-                off = (t // K7) * XK + t % K7
-                ek = e[:, k * CHQ : (k + 1) * CHQ]
-                ek3 = ek.rearrange("p (h w) -> p h w", w=W)
-                pg = stage.tile([P, CHQ], F32, name="pg", bufs=6)
-                g0 = 3 * XL + c * XWIN + off
-                nc.gpsimd.tensor_tensor(
-                    out=pg[:].rearrange("p (h w) -> p h w", w=W),
-                    in0=ek3,
-                    in1=xp[:, g0 : g0 + XWIN].rearrange("p (h k) -> p h k", k=XK)[:, :, 0:W],
-                    op=ALU.mult,
-                )
-                pv = stage.tile([P, 3 * CHQ], F32, name="pv", bufs=6)
-                nc.vector.tensor_tensor(
-                    out=pv[:, 0 : 2 * CHQ].rearrange("p (j h w) -> p j h w", j=2, w=W),
-                    in0=xw0[:]
-                    .rearrange("p (j n) -> p j n", j=2)[:, :, off : off + XWIN]
-                    .rearrange("p j (h k) -> p j h k", k=XK)[:, :, :, 0:W],
-                    in1=ek3.unsqueeze(1).to_broadcast([P, 2, CHR, W]),
-                    op=ALU.mult,
-                )
-                nc.vector.tensor_tensor(
-                    out=pv[:, 2 * CHQ : 3 * CHQ].rearrange("p (h w) -> p h w", w=W),
-                    in0=xw1[:, off : off + XWIN].rearrange("p (h k) -> p h k", k=XK)[:, :, 0:W],
-                    in1=ek3,
-                    op=ALU.mult,
-                )
+                pv, pg = pr_of[u][k]
                 first = t == 0
                 last = t == KK - 1
                 for qb in range(QB):
-                    add_block(accz, qb, ek[:, qb * P : (qb + 1) * P], first and qb == 0, last and qb == QB - 1)
-                for i in range(2 * QB):
-                    add_block(acc_a, i, pv[:, i * P : (i + 1) * P], first and i == 0, last and i == 2 * QB - 1)
-                for qb in range(QB):
-                    add_block(acc_b, qb, pv[:, (2 * QB + qb) * P : (2 * QB + qb + 1) * P], first and qb == 0, False)
-                for qb in range(QB):
-                    add_block(acc_b, QB + qb, pg[:, qb * P : (qb + 1) * P], False, last and qb == QB - 1)
+                    q0 = k * CHQ + qb * P
+                    add_block(accz, qb, e_of[u][:, q0 : q0 + P], first and qb == 0, last and qb == QB - 1)
+                for bank, pr in ((acc_a, pv), (acc_b, pg)):
+                    for i in range(2 * QB):
+                        add_block(bank, i, pr[:, i * P : (i + 1) * P], first and i == 0, last and i == 2 * QB - 1)
 
-        def finish(c):
+        def finish_vector(c):
             accz, acc_a, acc_b = acc_of[c]
-            rz = stage.tile([P, CHQ], F32, name="rz")
+            rz = stage.tile([P, CHQ], F32, name="rz", bufs=2)
             nc.vector.reciprocal(out=rz[:], in_=accz[:, 0:CHQ])
-            osb = stage.tile([P, CC * CHQ], F32, name="osb", bufs=2)
-            for i, bank in enumerate((acc_a, acc_b)):
-                on = stage.tile([P, 512], F32, name="on")
+            ons = []
+            for bank in (acc_a, acc_b):
+                on = stage.tile([P, 512], F32, name="on", bufs=2)
                 nc.vector.tensor_tensor(
                     out=on[:].rearrange("p (j n) -> p j n", j=2),
                     in0=bank[:].rearrange("p (j n) -> p j n", j=2),
                     in1=rz[:].unsqueeze(1).to_broadcast([P, 2, CHQ]),
                     op=ALU.mult,
                 )
+                ons.append(on)
+            return ons
+
+        def finish_store(c, ons):
+            osb = stage.tile([P, CC * CHQ], F32, name="osb", bufs=2)
+            for i, on in enumerate(ons):
                 pb = psum.tile([P, 512], F32, tag="mm", name="pb")
                 for s in range(4):
                     nc.tensor.transpose(pb[:, s * P : (s + 1) * P], on[:, s * P : (s + 1) * P], ident[:])
@@ -331,19 +370,61 @@ def tile_involution_kernel(tc, x, w_reduce, b_reduce, w_span, b_span, out):
                 in_=osb[:].rearrange("p (j q) -> p j q", j=CC),
             )
 
+        done = 0
+        for a in range(KK // WS_TAPS):
+            prepare_ws(a)
+            while done < LEAD and units[done][1][-1] < (a + 1) * WS_TAPS:
+                stage_pass(done)
+                stage_max(done, 0)
+                stage_max(done, 1)
+                stage_copy(done)
+                if units[done][1][-1] == KK - 1:
+                    merge_max(units[done][0])
+                done += 1
+        while done < LEAD:
+            stage_pass(done)
+            stage_max(done, 0)
+            stage_max(done, 1)
+            stage_copy(done)
+            done += 1
+
         with tc.manual_schedule():
+            max_to_psum(0)
             load_windows(0)
-            stage_pass(0)
-            stage_pass(1)
+            stage_pass(LEAD)
+            stage_sub(0)
             stage_exp(0)
-            for u in range(n_units):
-                if u + 2 < n_units:
-                    stage_pass(u + 2)
-                if u + 1 < n_units:
-                    stage_exp(u + 1)
-                stage_sum(u)
-                c, taps = units[u]
+            stage_sub(1)
+            ons = None
+            for n in range(n_units):
+                c, taps = units[n]
+                if n + LEAD + 1 < n_units:
+                    stage_pass(n + LEAD + 1)
+                cs, ts = units[min(n + 2, n_units - 1)]
+                if n + 2 < n_units and ts[0] == 0:
+                    max_to_psum(cs)
+                if n + 1 < n_units:
+                    stage_exp(n + 1)
+                ahead = n + LEAD < n_units
+                if ahead:
+                    stage_max(n + LEAD, 0)
+                stage_product(n, 0)
+                if ahead:
+                    stage_max(n + LEAD, 1)
+                    stage_copy(n + LEAD)
+                stage_product(n, 1)
+                if n + 2 < n_units:
+                    stage_sub(n + 2)
+                if ahead and units[n + LEAD][1][-1] == KK - 1:
+                    merge_max(units[n + LEAD][0])
+                if ons is not None:
+                    ons = finish_vector(c - 1)
+                if taps[-1] == KK - 1 and c + 1 < NCH:
+                    load_windows(c + 1)
+                stage_add(n)
+                if ons is not None:
+                    finish_store(c - 1, ons)
+                    ons = None
                 if taps[-1] == KK - 1:
-                    finish(c)
-                    if c + 1 < NCH:
-                        load_windows(c + 1)
+                    ons = []
+            finish_store(NCH - 1, finish_vector(NCH - 1))

@@ -197,7 +197,9 @@ def tile_involution_kernel(tc, x, w_reduce, b_reduce, w_span, b_span, out):
         xw_of = {}
         mm_of = {}
         ms_of = {}
-        mp_of = {}
+        side = pacc.tile([P, 512], F32, name="side")
+        mp = side[:, 0:CHQ]
+        xw2 = side[:, CHQ : 2 * CHQ].bitcast(BF16)
 
         def load_windows(c):
             xw0 = pacc.tile([P, 1024], BF16, name="xw0")
@@ -210,6 +212,13 @@ def tile_involution_kernel(tc, x, w_reduce, b_reduce, w_span, b_span, out):
                     stop=True,
                 )
             xw_of[c] = xw0
+            nc.tensor.matmul(
+                out=xw2,
+                lhsT=ident_bf[:],
+                rhs=xp[:, 2 * XL + c * XWIN : 2 * XL + c * XWIN + 512],
+                start=True,
+                stop=True,
+            )
 
         def stage_pass(u):
             c, taps = units[u]
@@ -254,9 +263,7 @@ def tile_involution_kernel(tc, x, w_reduce, b_reduce, w_span, b_span, out):
             ms_of[c] = ms
 
         def max_to_psum(c):
-            mp = pacc.tile([P, CHQ], F32, name="mp")
-            nc.tensor.matmul(out=mp[:], lhsT=ident[:], rhs=ms_of[c][:], start=True, stop=True)
-            mp_of[c] = mp
+            nc.tensor.matmul(out=mp, lhsT=ident[:], rhs=ms_of[c][:], start=True, stop=True)
 
         def stage_sub(u):
             c, taps = units[u]
@@ -265,7 +272,7 @@ def tile_involution_kernel(tc, x, w_reduce, b_reduce, w_span, b_span, out):
             nc.vector.tensor_tensor(
                 out=kb3,
                 in0=kb3,
-                in1=mp_of[c][:].unsqueeze(1).to_broadcast([P, n, CHQ]),
+                in1=mp.unsqueeze(1).to_broadcast([P, n, CHQ]),
                 op=ALU.subtract,
             )
 
@@ -289,32 +296,39 @@ def tile_involution_kernel(tc, x, w_reduce, b_reduce, w_span, b_span, out):
                 return
             t = taps[k]
             off = (t // K7) * XK + t % K7
-            ek4 = (
-                e_of[u][:, k * CHQ : (k + 1) * CHQ]
-                .rearrange("p (h w) -> p h w", w=W)
-                .unsqueeze(1)
-                .to_broadcast([P, 2, CHR, W])
-            )
+            ek3 = e_of[u][:, k * CHQ : (k + 1) * CHQ].rearrange("p (h w) -> p h w", w=W)
+            ek4 = ek3.unsqueeze(1).to_broadcast([P, 2, CHR, W])
+            nv = 2 + k
+            ng = CC - nv
             pg = stage.tile([P, 2 * CHQ], F32, name="pg", bufs=5)
+            pv = stage.tile([P, 3 * CHQ], F32, name="pv", bufs=5)
             g0 = c * XWIN + off
             nc.gpsimd.tensor_tensor(
-                out=pg[:].rearrange("p (j h w) -> p j h w", j=2, w=W),
-                in0=ek4,
+                out=pg[:, 0 : ng * CHQ].rearrange("p (j h w) -> p j h w", j=ng, w=W),
+                in0=ek3.unsqueeze(1).to_broadcast([P, ng, CHR, W]),
                 in1=xp[:]
-                .rearrange("p (j n) -> p j n", j=CC)[:, 2:4, g0 : g0 + XWIN]
+                .rearrange("p (j n) -> p j n", j=CC)[:, nv:CC, g0 : g0 + XWIN]
                 .rearrange("p j (h k) -> p j h k", k=XK)[:, :, :, 0:W],
                 op=ALU.mult,
             )
-            pv = stage.tile([P, 2 * CHQ], F32, name="pv", bufs=5)
             nc.vector.tensor_tensor(
-                out=pv[:].rearrange("p (j h w) -> p j h w", j=2, w=W),
+                out=pv[:, 0 : 2 * CHQ].rearrange("p (j h w) -> p j h w", j=2, w=W),
                 in0=xw_of[c][:]
                 .rearrange("p (j n) -> p j n", j=2)[:, :, off : off + XWIN]
                 .rearrange("p j (h k) -> p j h k", k=XK)[:, :, :, 0:W],
                 in1=ek4,
                 op=ALU.mult,
             )
-            pr_of[u].append((pv, pg))
+            if nv == 3:
+                nc.vector.tensor_tensor(
+                    out=pv[:, 2 * CHQ : 3 * CHQ].rearrange("p (h w) -> p h w", w=W),
+                    in0=xw2[:, off : off + XWIN].rearrange("p (h k) -> p h k", k=XK)[:, :, 0:W],
+                    in1=ek3,
+                    op=ALU.mult,
+                )
+            blocks = [pv[:, i * P : (i + 1) * P] for i in range(nv * QB)]
+            blocks += [pg[:, i * P : (i + 1) * P] for i in range(ng * QB)]
+            pr_of[u].append(blocks)
 
         def add_block(bank, slot, block, first, last):
             nc.tensor.matmul(
@@ -332,15 +346,15 @@ def tile_involution_kernel(tc, x, w_reduce, b_reduce, w_span, b_span, out):
                 acc_of[c] = [pacc.tile([P, 512], F32, tag="acc%d" % i, name="acc") for i in range(3)]
             accz, acc_a, acc_b = acc_of[c]
             for k, t in enumerate(taps):
-                pv, pg = pr_of[u][k]
+                blocks = pr_of[u][k]
                 first = t == 0
                 last = t == KK - 1
                 for qb in range(QB):
                     q0 = k * CHQ + qb * P
                     add_block(accz, qb, e_of[u][:, q0 : q0 + P], first and qb == 0, last and qb == QB - 1)
-                for bank, pr in ((acc_a, pv), (acc_b, pg)):
+                for b, bank in enumerate((acc_a, acc_b)):
                     for i in range(2 * QB):
-                        add_block(bank, i, pr[:, i * P : (i + 1) * P], first and i == 0, last and i == 2 * QB - 1)
+                        add_block(bank, i, blocks[2 * QB * b + i], first and i == 0, last and i == 2 * QB - 1)
 
         def finish_vector(c):
             accz, acc_a, acc_b = acc_of[c]

@@ -28,7 +28,9 @@ NCH = 4
 CHR = H // NCH
 CHQ = CHR * W
 QB = CHQ // P
-WS_TAPS = 7
+WS_TAPS = 8
+NCOPY = 8
+XROWS = HP * W
 XK = W + PAD
 XL = 1352
 XWIN = CHR * XK
@@ -39,155 +41,19 @@ def tile_involution_kernel(tc, x, w_reduce, b_reduce, w_span, b_span, out):
     nc = tc.nc
     with ExitStack() as ctx:
         const = ctx.enter_context(tc.tile_pool(name="const", bufs=1))
-        wsp = ctx.enter_context(tc.tile_pool(name="wsp", bufs=3))
         stage = ctx.enter_context(tc.tile_pool(name="stage", bufs=3))
         psum = ctx.enter_context(tc.psum_pool(name="psum", bufs=3))
         pacc = ctx.enter_context(tc.psum_pool(name="pacc", bufs=1))
 
-        x_sb = const.tile([P, CC * HW], BF16)
-        nc.sync.dma_start(out=x_sb[:], in_=x[0].rearrange("(g j) h w -> g (j h w)", j=CC))
-        wr_sb = const.tile([P, 4 * 512], BF16)
-        nc.sync.dma_start(
-            out=wr_sb[:].rearrange("p (u f) -> p u f", u=2),
-            in_=w_reduce.rearrange("(u p e) c -> p u (e c)", u=2, e=2),
-        )
-        br_b = const.tile([P, 4], BF16)
-        bs_b = const.tile([P, KK], BF16)
-        with nc.allow_non_contiguous_dma(reason="two small bias vectors"):
-            nc.sync.dma_start(
-                out=br_b[:].rearrange("p (u e) -> p u e", u=2),
-                in_=b_reduce.rearrange("(u p e) -> p u e", u=2, e=2),
-            )
-            nc.sync.dma_start(out=bs_b[:], in_=b_span.rearrange("(g t) -> g t", t=KK))
-        ws_view = w_span.rearrange("(g t) r -> g t r", t=KK)
-        ws_tiles = []
-
-        def load_ws(a):
-            ws_sb = wsp.tile([P, WS_TAPS * R], BF16, name="ws_sb")
-            nc.sync.dma_start(
-                out=ws_sb[:].rearrange("p (t r) -> p t r", t=WS_TAPS),
-                in_=ws_view[:, a * WS_TAPS : (a + 1) * WS_TAPS, :],
-            )
-            ws_tiles.append(ws_sb)
-
-        for a in range(3):
-            load_ws(a)
-
-        ident = const.tile([P, P], F32)
-        make_identity(nc, ident[:])
-
-        br = const.tile([P, 4], F32)
-        nc.vector.tensor_copy(out=br[:], in_=br_b[:])
-        bs = const.tile([P, KK], F32)
-        nc.vector.tensor_copy(out=bs[:], in_=bs_b[:])
-
-        ident_bf = const.tile([P, P], BF16)
-        make_identity(nc, ident_bf[:])
-        xp = const.tile([P, CC * XL], BF16)
-        nc.gpsimd.memset(xp[:], 0.0)
-        x0 = PAD + PAD * XK
-        nc.gpsimd.tensor_copy(
-            out=xp[:]
-            .rearrange("p (j n) -> p j n", j=CC)[:, :, x0 : x0 + H * XK]
-            .rearrange("p j (h k) -> p j h k", k=XK)[:, :, :, 0:W],
-            in_=x_sb[:].rearrange("p (j h w) -> p j h w", j=CC, w=W),
-        )
-
-        gx = const.tile([P, HW * 4], BF16, tag="grp", align_bytes=64)
-        nc.vector.tensor_copy(
-            out=gx[:].rearrange("p (q j) -> p q j", j=4),
-            in_=x_sb[:].rearrange("p (j q) -> p q j", j=4),
-        )
-        x_codes = const.tile([P, HW], U32, align_bytes=64)
-        x_scl = const.tile([P, HW], U8, align_bytes=64)
-        nc.vector.quantize_mx(out=x_codes[:].bitcast(FP8X4), scales=x_scl[:], in_=gx[:])
-
-        wr32 = wr_sb[:].bitcast(F32).rearrange("p (a w v) -> p a v w", a=4, v=2)
-        gw = const.tile([P, 4 * P * 4], BF16, align_bytes=64)
-        gw32 = gw[:].bitcast(F32).rearrange("p (a r v) -> p a r v", a=4, v=2)
-        for b in range(2):
-            tp = pacc.tile([P, 512], F32, tag="acc%d" % b, name="tp")
-            for a2 in range(2):
-                for v in range(2):
-                    nc.tensor.transpose(
-                        tp[:, (a2 * 2 + v) * P : (a2 * 2 + v + 1) * P], wr32[:, 2 * b + a2, v, :], ident[:]
-                    )
-            nc.scalar.copy(
-                out=gw32[:, 2 * b : 2 * b + 2, :, :],
-                in_=tp[:].rearrange("p (a v r) -> p a r v", a=2, v=2),
-            )
-        wr_codes = const.tile([P, 4 * P], U32, align_bytes=64)
-        wr_scl = const.tile([P, 4 * P], U8, align_bytes=64)
-        nc.vector.quantize_mx(out=wr_codes[:].bitcast(FP8X4), scales=wr_scl[:], in_=gw[:])
-
-        red_t = const.tile([P, 4 * HW], BF16)
-        for a in range(4):
-            for hf in range(2):
-                ps = psum.tile([P, 512], F32, tag="mm", name="ps")
-                nc.tensor.matmul_mx(
-                    out=ps[:],
-                    lhsT=wr_codes[:, a * P : (a + 1) * P].bitcast(FP8X4),
-                    lhsT_scale=wr_scl[:, a * P : (a + 1) * P],
-                    rhs=x_codes[:, hf * 512 : (hf + 1) * 512].bitcast(FP8X4),
-                    rhs_scale=x_scl[:, hf * 512 : (hf + 1) * 512],
-                    start=True,
-                    stop=True,
-                )
-                nc.scalar.activation(
-                    out=red_t[:, a * HW + hf * 512 : a * HW + (hf + 1) * 512],
-                    in_=ps[:],
-                    func=ACT.Relu,
-                    bias=br[:, a : a + 1],
-                    scale=1.0,
-                )
-        gr = const.tile([P, HW * 4], BF16, tag="grp", align_bytes=64)
-        nc.vector.tensor_copy(
-            out=gr[:].rearrange("p (q a) -> p q a", a=4),
-            in_=red_t[:].rearrange("p (a q) -> p q a", a=4),
-        )
-        red_codes = const.tile([P, HW], U32, align_bytes=64)
-        red_scl = const.tile([P, HW], U8, align_bytes=64)
-        nc.vector.quantize_mx(out=red_codes[:].bitcast(FP8X4), scales=red_scl[:], in_=gr[:])
-
-        ws_codes = const.tile([P, KK * P], U32, align_bytes=64)
-        ws_scl = const.tile([P, KK * P], U8, align_bytes=64)
-        n_banks = [0]
-
-        def prepare_ws(a):
-            ws32 = ws_tiles[a][:].bitcast(F32).rearrange("p (t u w) -> p t u w", t=WS_TAPS, u=2)
-            t0 = 0
-            for n in (4, 2, 1):
-                gws = stage.tile([P, 4 * P * 4], BF16, name="gws", align_bytes=64)
-                gws32 = gws[:].bitcast(F32).rearrange("p (t g u) -> p t g u", t=4, u=2)
-                for b0 in range(0, n, 2):
-                    nb = min(2, n - b0)
-                    tp = pacc.tile([P, 512], F32, tag="acc%d" % (n_banks[0] % 3), name="tp")
-                    n_banks[0] += 1
-                    for tl in range(nb):
-                        for u in range(2):
-                            nc.tensor.transpose(
-                                tp[:, (tl * 2 + u) * P : (tl * 2 + u + 1) * P],
-                                ws32[:, t0 + b0 + tl, u, :],
-                                ident[:],
-                            )
-                    nc.scalar.copy(
-                        out=gws32[:, b0 : b0 + nb, :, :],
-                        in_=tp[:].rearrange("p (t u g) -> p t g u", t=2, u=2)[:, 0:nb, :, :],
-                    )
-                tg = a * WS_TAPS + t0
-                nc.vector.quantize_mx(
-                    out=ws_codes[:, tg * P : (tg + n) * P].bitcast(FP8X4),
-                    scales=ws_scl[:, tg * P : (tg + n) * P],
-                    in_=gws[:, 0 : n * P * 4],
-                )
-                t0 += n
-            if a + 3 < KK // WS_TAPS:
-                load_ws(a + 3)
-
         out_v = out[0].rearrange("(g j) h w -> g j (h w)", j=CC)
-        units = [(c, [t for t in (t0, t0 + 1) if t < KK]) for c in range(NCH) for t0 in range(0, KK, 2)]
+        pairs = []
+        for i in range(0, K7, 2):
+            rows = range(i, min(i + 2, K7))
+            pairs += [[r * K7 + j, r * K7 + j + 1] for r in rows for j in range(0, K7 - 1, 2)]
+            pairs.append([r * K7 + K7 - 1 for r in rows])
+        upc = len(pairs)
+        units = [(c, taps) for c in range(NCH) for taps in pairs]
         n_units = len(units)
-        upc = n_units // NCH
         LEAD = upc + 2
         ps_of = {}
         kb_of = {}
@@ -240,11 +106,11 @@ def tile_involution_kernel(tc, x, w_reduce, b_reduce, w_span, b_span, out):
             if k >= len(taps):
                 return
             t = taps[k]
-            if t == 0:
+            if u % upc == 0 and k == 0:
                 mm_of[c] = stage.tile([P, 512], F32, name="mm", bufs=2)
             mk = mm_of[c][:, k * CHQ : (k + 1) * CHQ]
             pk = ps_of[u][:, k * CHQ : (k + 1) * CHQ]
-            if t < 2:
+            if u % upc == 0:
                 nc.vector.tensor_scalar_add(out=mk, in0=pk, scalar1=bs[:, t : t + 1])
             else:
                 nc.vector.scalar_tensor_tensor(
@@ -278,7 +144,7 @@ def tile_involution_kernel(tc, x, w_reduce, b_reduce, w_span, b_span, out):
 
         def stage_exp(u):
             c, taps = units[u]
-            e = stage.tile([P, 512], F32, name="e", bufs=4)
+            e = main.tile([P, 512], F32, name="e", bufs=4)
             for k, t in enumerate(taps):
                 nc.scalar.activation(
                     out=e[:, k * CHQ : (k + 1) * CHQ],
@@ -288,47 +154,55 @@ def tile_involution_kernel(tc, x, w_reduce, b_reduce, w_span, b_span, out):
                     scale=1.0,
                 )
             e_of[u] = e
-            pr_of[u] = []
 
-        def stage_product(u, k):
+        def vector_has_channel_2(u):
+            return u % 5 == 4
+
+        def product_gpsimd(u):
+            c, taps = units[u]
+            n = len(taps)
+            j0 = 1 if vector_has_channel_2(u) else 0
+            ng = 2 - j0
+            pg = main.tile([P, 4 * CHQ], F32, name="pg", bufs=4)
+            s0 = taps[0] % K7
+            q0 = (taps[0] // K7 + c * CHR) * W
+            nc.gpsimd.tensor_tensor(
+                out=pg[:, 0 : n * ng * CHQ].rearrange("p (k j q) -> p k j q", k=n, j=ng),
+                in0=e_of[u][:, 0 : n * CHQ]
+                .rearrange("p (k q) -> p k q", k=n)
+                .unsqueeze(2)
+                .to_broadcast([P, n, ng, CHQ]),
+                in1=xs[:].rearrange("p (s j q) -> p s j q", s=NCOPY, j=2)[:, s0 : s0 + n, j0:2, q0 : q0 + CHQ],
+                op=ALU.mult,
+            )
+            pr_of[u] = [[pg[:, (k * ng * QB + i) * P : (k * ng * QB + i + 1) * P] for i in range(ng * QB)] for k in range(n)]
+
+        def product_vector(u, k):
             c, taps = units[u]
             if k >= len(taps):
                 return
-            t = taps[k]
-            off = (t // K7) * XK + t % K7
+            off = (taps[k] // K7) * XK + taps[k] % K7
             ek3 = e_of[u][:, k * CHQ : (k + 1) * CHQ].rearrange("p (h w) -> p h w", w=W)
-            ek4 = ek3.unsqueeze(1).to_broadcast([P, 2, CHR, W])
-            nv = 2 + k
-            ng = CC - nv
-            pg = stage.tile([P, 2 * CHQ], F32, name="pg", bufs=5)
-            pv = stage.tile([P, 3 * CHQ], F32, name="pv", bufs=5)
-            g0 = c * XWIN + off
-            nc.gpsimd.tensor_tensor(
-                out=pg[:, 0 : ng * CHQ].rearrange("p (j h w) -> p j h w", j=ng, w=W),
-                in0=ek3.unsqueeze(1).to_broadcast([P, ng, CHR, W]),
-                in1=xp[:]
-                .rearrange("p (j n) -> p j n", j=CC)[:, nv:CC, g0 : g0 + XWIN]
-                .rearrange("p j (h k) -> p j h k", k=XK)[:, :, :, 0:W],
-                op=ALU.mult,
-            )
+            pv = main.tile([P, 2 * CHQ], F32, name="pv", bufs=6)
             nc.vector.tensor_tensor(
-                out=pv[:, 0 : 2 * CHQ].rearrange("p (j h w) -> p j h w", j=2, w=W),
+                out=pv[:].rearrange("p (j h w) -> p j h w", j=2, w=W),
                 in0=xw_of[c][:]
                 .rearrange("p (j n) -> p j n", j=2)[:, :, off : off + XWIN]
                 .rearrange("p j (h k) -> p j h k", k=XK)[:, :, :, 0:W],
-                in1=ek4,
+                in1=ek3.unsqueeze(1).to_broadcast([P, 2, CHR, W]),
                 op=ALU.mult,
             )
-            if nv == 3:
+            blocks = [pv[:, i * P : (i + 1) * P] for i in range(2 * QB)]
+            if vector_has_channel_2(u):
+                pv2 = main.tile([P, CHQ], F32, name="pv2", bufs=4)
                 nc.vector.tensor_tensor(
-                    out=pv[:, 2 * CHQ : 3 * CHQ].rearrange("p (h w) -> p h w", w=W),
+                    out=pv2[:].rearrange("p (h w) -> p h w", w=W),
                     in0=xw2[:, off : off + XWIN].rearrange("p (h k) -> p h k", k=XK)[:, :, 0:W],
                     in1=ek3,
                     op=ALU.mult,
                 )
-            blocks = [pv[:, i * P : (i + 1) * P] for i in range(nv * QB)]
-            blocks += [pg[:, i * P : (i + 1) * P] for i in range(ng * QB)]
-            pr_of[u].append(blocks)
+                blocks += [pv2[:, i * P : (i + 1) * P] for i in range(QB)]
+            pr_of[u][k] = blocks + pr_of[u][k]
 
         def add_block(bank, slot, block, first, last):
             nc.tensor.matmul(
@@ -342,7 +216,7 @@ def tile_involution_kernel(tc, x, w_reduce, b_reduce, w_span, b_span, out):
 
         def stage_add(u):
             c, taps = units[u]
-            if taps[0] == 0:
+            if u % upc == 0:
                 acc_of[c] = [pacc.tile([P, 512], F32, tag="acc%d" % i, name="acc") for i in range(3)]
             accz, acc_a, acc_b = acc_of[c]
             for k, t in enumerate(taps):
@@ -356,89 +230,336 @@ def tile_involution_kernel(tc, x, w_reduce, b_reduce, w_span, b_span, out):
                     for i in range(2 * QB):
                         add_block(bank, i, blocks[2 * QB * b + i], first and i == 0, last and i == 2 * QB - 1)
 
-        def finish_vector(c):
+        def empty_sums(c):
             accz, acc_a, acc_b = acc_of[c]
-            rz = stage.tile([P, CHQ], F32, name="rz", bufs=2)
-            nc.vector.reciprocal(out=rz[:], in_=accz[:, 0:CHQ])
-            ons = []
+            zs = main.tile([P, CHQ], F32, name="zs", bufs=1)
+            nc.scalar.copy(out=zs[:], in_=accz[:, 0:CHQ])
+            sums = [zs]
             for bank in (acc_a, acc_b):
-                on = stage.tile([P, 512], F32, name="on", bufs=2)
-                nc.vector.tensor_tensor(
-                    out=on[:].rearrange("p (j n) -> p j n", j=2),
-                    in0=bank[:].rearrange("p (j n) -> p j n", j=2),
-                    in1=rz[:].unsqueeze(1).to_broadcast([P, 2, CHQ]),
-                    op=ALU.mult,
-                )
-                ons.append(on)
-            return ons
+                sm = main.tile([P, 512], F32, name="sm", bufs=2)
+                nc.scalar.copy(out=sm[:], in_=bank[:])
+                sums.append(sm)
+            osb = main.tile([P, CC * CHQ], F32, name="osb", bufs=2)
+            sums.append(osb)
+            return sums
 
-        def finish_store(c, ons):
-            osb = stage.tile([P, CC * CHQ], F32, name="osb", bufs=2)
-            for i, on in enumerate(ons):
-                pb = psum.tile([P, 512], F32, tag="mm", name="pb")
-                for s in range(4):
-                    nc.tensor.transpose(pb[:, s * P : (s + 1) * P], on[:, s * P : (s + 1) * P], ident[:])
-                nc.scalar.copy(out=osb[:, i * 512 : (i + 1) * 512], in_=pb[:])
+        def turn_back(block):
+            tb = psum.tile([P, 512], F32, tag="mm", name="tb")
+            for s in range(block.shape[1] // P):
+                nc.tensor.transpose(tb[:, s * P : (s + 1) * P], block[:, s * P : (s + 1) * P], ident[:])
+            return tb
+
+        def reciprocal_z(tb):
+            rz = main.tile([P, CHQ], F32, name="rz", bufs=1)
+            nc.vector.reciprocal(out=rz[:], in_=tb[:, 0:CHQ])
+            return rz
+
+        def scale_pair(c, i, tb, rz, osb):
+            nc.vector.tensor_tensor(
+                out=osb[:, i * 512 : (i + 1) * 512].rearrange("p (j n) -> p j n", j=2),
+                in0=tb[:].rearrange("p (j n) -> p j n", j=2),
+                in1=rz[:].unsqueeze(1).to_broadcast([P, 2, CHQ]),
+                op=ALU.mult,
+            )
             nc.sync.dma_start(
-                out=out_v[:, :, c * CHQ : (c + 1) * CHQ],
-                in_=osb[:].rearrange("p (j q) -> p j q", j=CC),
+                out=out_v[:, 2 * i : 2 * i + 2, c * CHQ : (c + 1) * CHQ],
+                in_=osb[:, i * 512 : (i + 1) * 512].rearrange("p (j q) -> p j q", j=2),
             )
 
-        done = 0
-        for a in range(KK // WS_TAPS):
-            prepare_ws(a)
-            while done < LEAD and units[done][1][-1] < (a + 1) * WS_TAPS:
-                stage_pass(done)
-                stage_max(done, 0)
-                stage_max(done, 1)
-                stage_copy(done)
-                if units[done][1][-1] == KK - 1:
-                    merge_max(units[done][0])
-                done += 1
-        while done < LEAD:
-            stage_pass(done)
-            stage_max(done, 0)
-            stage_max(done, 1)
-            stage_copy(done)
-            done += 1
+        def stage_kern(u):
+            stage_pass(u)
+            stage_max(u, 0)
+            stage_max(u, 1)
+            stage_copy(u)
+
+        with tc.tile_pool(name="head", bufs=1) as head:
+            ident = const.tile([P, P], F32)
+            make_identity(nc, ident[:])
+            ident_bf = const.tile([P, P], BF16)
+            make_identity(nc, ident_bf[:])
+
+            wr_sb = head.tile([P, 4 * 512], BF16)
+            x_half = [const.tile([P, CC * 512], BF16, name="xh%d" % i) for i in range(2)]
+            br_b = const.tile([P, 4], BF16)
+            bs_b = const.tile([P, KK], BF16)
+            br = const.tile([P, 4], F32)
+            bs = const.tile([P, KK], F32)
+            xp = const.tile([P, 3 * XL], BF16)
+            xs = const.tile([P, NCOPY * 2 * XROWS], BF16)
+            xs5 = xs[:].rearrange("p (s j h w) -> p s j h w", s=NCOPY, j=2, w=W)
+            gw = head.tile([P, 4 * P * 4], BF16, align_bytes=64)
+            wr_codes = const.tile([P, 4 * P], U32, align_bytes=64)
+            wr_scl = const.tile([P, 4 * P], U8, align_bytes=64)
+            x_codes = const.tile([P, HW], U32, align_bytes=64)
+            x_scl = const.tile([P, HW], U8, align_bytes=64)
+            red_codes = const.tile([P, HW], U32, align_bytes=64)
+            red_scl = const.tile([P, HW], U8, align_bytes=64)
+            ws_codes = const.tile([P, KK * P], U32, align_bytes=64)
+            ws_scl = const.tile([P, KK * P], U8, align_bytes=64)
+            groups = {}
+            red_of = {}
+            ws_tiles = []
+            gws_of = {}
+            x_view = x[0].rearrange("(g j) h w -> g j (h w)", j=CC)
+            ws_view = w_span.rearrange("(g t) r -> g t r", t=KK)
+
+            def load_x(i):
+                nc.sync.dma_start(
+                    out=x_half[i][:].rearrange("p (j q) -> p j q", j=CC), in_=x_view[:, :, i * 512 : (i + 1) * 512]
+                )
+
+            def load_ws(a):
+                n = min(WS_TAPS, KK - a * WS_TAPS)
+                ws_sb = head.tile([P, WS_TAPS * R], BF16, name="ws_sb", bufs=4)
+                nc.sync.dma_start(
+                    out=ws_sb[:, 0 : n * R].rearrange("p (t r) -> p t r", t=n),
+                    in_=ws_view[:, a * WS_TAPS : a * WS_TAPS + n, :],
+                )
+                ws_tiles.append(ws_sb)
+
+            def fill_xp(i):
+                x0 = PAD + (PAD + i * H // 2) * XK
+                nc.gpsimd.tensor_scalar(
+                    out=xp[:]
+                    .rearrange("p (j n) -> p j n", j=3)[:, :, x0 : x0 + H // 2 * XK]
+                    .rearrange("p j (h k) -> p j h k", k=XK)[:, :, :, 0:W],
+                    in0=x_half[i][:].rearrange("p (j h w) -> p j h w", j=CC, w=W)[:, 0:3, :, :],
+                    scalar1=1.0,
+                    scalar2=0.0,
+                    op0=ALU.mult,
+                    op1=ALU.add,
+                )
+
+            def zero_xs_rows():
+                for rows in (slice(0, PAD), slice(HP - PAD - 1, HP)):
+                    nc.gpsimd.memset(
+                        xs[:].rearrange("p (n h w) -> p n (h w)", h=HP, w=W)[:, :, rows.start * W : rows.stop * W], 0.0
+                    )
+
+            def zero_xs_columns():
+                for s in range(NCOPY):
+                    d = min(s, K7 - 1) - PAD
+                    if d != 0:
+                        cols = slice(0, 4) if d < 0 else slice(W - 4, W)
+                        nc.vector.memset(xs5[:, s, :, PAD : HP - PAD - 1, cols], 0.0)
+
+            def xs_views(s, h0, h1):
+                i = h0 // (H // 2)
+                d = min(s, K7 - 1) - PAD
+                w0, w1 = max(0, -d), min(W, W - d)
+                r0 = h0 + PAD - s // K7
+                src = x_half[i][:].rearrange("p (j h w) -> p j h w", j=CC, w=W)
+                b = i * (H // 2)
+                return xs5[:, s, :, r0 : r0 + h1 - h0, w0:w1], src[:, 2:4, h0 - b : h1 - b, w0 + d : w1 + d]
+
+            def fill_xs_gpsimd(s, h0, h1):
+                dst, src = xs_views(s, h0, h1)
+                nc.gpsimd.tensor_scalar(out=dst, in0=src, scalar1=1.0, scalar2=0.0, op0=ALU.mult, op1=ALU.add)
+
+            def fill_xs_scalar(s, h0, h1):
+                dst, src = xs_views(s, h0, h1)
+                nc.scalar.copy(out=dst, in_=src)
+
+            def turn_wr(b):
+                wr32 = wr_sb[:].bitcast(F32).rearrange("p (a w v) -> p a v w", a=4, v=2)
+                gw32 = gw[:].bitcast(F32).rearrange("p (a r v) -> p a r v", a=4, v=2)
+                tp = pacc.tile([P, 512], F32, tag="acc%d" % b, name="tp")
+                for a2 in range(2):
+                    for v in range(2):
+                        nc.tensor.transpose(
+                            tp[:, (a2 * 2 + v) * P : (a2 * 2 + v + 1) * P], wr32[:, 2 * b + a2, v, :], ident[:]
+                        )
+                nc.scalar.copy(
+                    out=gw32[:, 2 * b : 2 * b + 2, :, :], in_=tp[:].rearrange("p (a v r) -> p a r v", a=2, v=2)
+                )
+
+            def group_part(key, src, engine_copy, q0, q1):
+                if key not in groups:
+                    groups[key] = const.tile([P, 4 * 512], BF16, tag="grp", name="grp", bufs=2, align_bytes=64)
+                engine_copy(
+                    out=groups[key][:].rearrange("p (q j) -> p q j", j=4)[:, q0:q1, :],
+                    in_=src.rearrange("p (j q) -> p q j", j=4)[:, q0:q1, :],
+                )
+
+            def quantise_half(codes, scl, i, grouped):
+                nc.vector.quantize_mx(
+                    out=codes[:, i * 512 : (i + 1) * 512].bitcast(FP8X4),
+                    scales=scl[:, i * 512 : (i + 1) * 512],
+                    in_=grouped[:],
+                )
+
+            def red_pass(i, a, on_vector):
+                if a == 0:
+                    red_of[i] = const.tile([P, 4 * 512], BF16, name="red", bufs=2)
+                ps = psum.tile([P, 512], F32, tag="mm", name="ps")
+                nc.tensor.matmul_mx(
+                    out=ps[:],
+                    lhsT=wr_codes[:, a * P : (a + 1) * P].bitcast(FP8X4),
+                    lhsT_scale=wr_scl[:, a * P : (a + 1) * P],
+                    rhs=x_codes[:, i * 512 : (i + 1) * 512].bitcast(FP8X4),
+                    rhs_scale=x_scl[:, i * 512 : (i + 1) * 512],
+                    start=True,
+                    stop=True,
+                )
+                dst = red_of[i][:, a * 512 : (a + 1) * 512]
+                if on_vector:
+                    nc.vector.tensor_scalar(
+                        out=dst, in0=ps[:], scalar1=br[:, a : a + 1], scalar2=0.0, op0=ALU.add, op1=ALU.max
+                    )
+                else:
+                    nc.scalar.activation(out=dst, in_=ps[:], func=ACT.Relu, bias=br[:, a : a + 1], scale=1.0)
+
+            n_groups = (KK + 3) // 4
+
+            def turn_ws(g):
+                n = min(4, KK - 4 * g)
+                ws32 = ws_tiles[4 * g // WS_TAPS][:].bitcast(F32).rearrange("p (t u w) -> p t u w", t=WS_TAPS, u=2)
+                gws = head.tile([P, 4 * P * 4], BF16, name="gws", bufs=3, align_bytes=64)
+                gws32 = gws[:].bitcast(F32).rearrange("p (t g u) -> p t g u", t=4, u=2)
+                for b in range((n + 1) // 2):
+                    nb = min(2, n - 2 * b)
+                    tp = pacc.tile([P, 512], F32, tag="acc%d" % ((2 * g + b) % 3), name="tp")
+                    for tl in range(nb):
+                        for u in range(2):
+                            nc.tensor.transpose(
+                                tp[:, (tl * 2 + u) * P : (tl * 2 + u + 1) * P],
+                                ws32[:, 4 * g % WS_TAPS + 2 * b + tl, u, :],
+                                ident[:],
+                            )
+                    copy = nc.vector.tensor_copy if b == 1 and g % 3 != 0 else nc.scalar.copy
+                    copy(
+                        out=gws32[:, 2 * b : 2 * b + nb, :, :],
+                        in_=tp[:].rearrange("p (t u g) -> p t g u", t=2, u=2)[:, 0:nb, :, :],
+                    )
+                gws_of[g] = gws
+                if (4 * g + 4) % WS_TAPS == 0 and (len(ws_tiles)) * WS_TAPS < KK:
+                    load_ws(len(ws_tiles))
+
+            def quantise_ws(g):
+                n = min(4, KK - 4 * g)
+                nc.vector.quantize_mx(
+                    out=ws_codes[:, 4 * g * P : (4 * g + n) * P].bitcast(FP8X4),
+                    scales=ws_scl[:, 4 * g * P : (4 * g + n) * P],
+                    in_=gws_of[g][:, 0 : n * P * 4],
+                )
+
+            with tc.manual_schedule():
+                nc.sync.dma_start(
+                    out=wr_sb[:].rearrange("p (u f) -> p u f", u=2),
+                    in_=w_reduce.rearrange("(u p e) c -> p u (e c)", u=2, e=2),
+                )
+                load_x(0)
+                with nc.allow_non_contiguous_dma(reason="two small bias vectors"):
+                    nc.sync.dma_start(
+                        out=br_b[:].rearrange("p (u e) -> p u e", u=2),
+                        in_=b_reduce.rearrange("(u p e) -> p u e", u=2, e=2),
+                    )
+                    load_ws(0)
+                    nc.sync.dma_start(out=bs_b[:], in_=b_span.rearrange("(g t) -> g t", t=KK))
+                load_ws(1)
+                load_x(1)
+                load_ws(2)
+                load_ws(3)
+
+                nc.gpsimd.memset(xp[:].bitcast(F32), 0.0)
+                zero_xs_rows()
+                zero_xs_columns()
+                nc.vector.memset(br[:], 0.0)
+                warm = const.tile([P, 1], F32)
+                nc.scalar.activation(out=warm[:], in_=br[:, 0:1], func=ACT.Exp, scale=1.0)
+                fill_xp(0)
+                fill_xp(1)
+                for s in range(NCOPY):
+                    fill_xs_gpsimd(s, 0, CHR + PAD)
+
+                turn_wr(0)
+                turn_wr(1)
+                group_part("x0", x_half[0][:], nc.vector.tensor_copy, 0, 512)
+                nc.vector.tensor_copy(out=br[:], in_=br_b[:])
+                nc.vector.quantize_mx(out=wr_codes[:].bitcast(FP8X4), scales=wr_scl[:], in_=gw[:])
+                quantise_half(x_codes, x_scl, 0, groups["x0"])
+                for a in range(4):
+                    red_pass(0, a, a % 2 == 1)
+                turn_ws(0)
+                nc.vector.tensor_copy(out=bs[:], in_=bs_b[:])
+                group_part("r0", red_of[0][:], nc.vector.tensor_copy, 0, 512)
+                turn_ws(1)
+                quantise_ws(0)
+                quantise_half(red_codes, red_scl, 0, groups["r0"])
+                done = 0
+                for g in range(1, n_groups + 2):
+                    if g + 1 < n_groups:
+                        turn_ws(g + 1)
+                    if g < n_groups:
+                        quantise_ws(g)
+                    while done < upc and units[done][1][-1] < 4 * g:
+                        stage_kern(done)
+                        done += 1
+                    if g == 4:
+                        load_windows(0)
+                merge_max(0)
+
+            late_steps = [
+                [lambda q0=q0: group_part("x1", x_half[1][:], nc.scalar.copy, q0, q0 + 256)] for q0 in (0, 256)
+            ]
+            late_steps.append([lambda: quantise_half(x_codes, x_scl, 1, groups["x1"])])
+            late_steps += [[lambda a=a: red_pass(1, a, False)] for a in range(4)]
+            late_steps += [
+                [lambda q0=q0: group_part("r1", red_of[1][:], nc.scalar.copy, q0, q0 + 256)] for q0 in (0, 256)
+            ]
+            late_steps.append([lambda: quantise_half(red_codes, red_scl, 1, groups["r1"])])
+            late_steps += [
+                [lambda s=s, h=h: fill_xs_scalar(s, *h) for h in ((CHR + PAD, H // 2), (H // 2, H))] for s in range(NCOPY)
+            ]
+        main = ctx.enter_context(tc.tile_pool(name="main", bufs=1))
 
         with tc.manual_schedule():
             max_to_psum(0)
-            load_windows(0)
-            stage_pass(LEAD)
             stage_sub(0)
             stage_exp(0)
             stage_sub(1)
-            ons = None
+            for u in range(upc, LEAD):
+                stage_kern(u)
+            stage_pass(LEAD)
             for n in range(n_units):
                 c, taps = units[n]
+                back = n % upc if c > 0 else upc
                 if n + LEAD + 1 < n_units:
                     stage_pass(n + LEAD + 1)
-                cs, ts = units[min(n + 2, n_units - 1)]
-                if n + 2 < n_units and ts[0] == 0:
-                    max_to_psum(cs)
+                if n + 2 < n_units and units[n + 2][1][0] == 0:
+                    max_to_psum(units[n + 2][0])
+                if back == 1:
+                    tb = turn_back(sums[0])
+                elif back in (2, 3):
+                    tb = turn_back(sums[back - 1])
                 if n + 1 < n_units:
                     stage_exp(n + 1)
+                if back == 0:
+                    sums = empty_sums(c - 1)
                 ahead = n + LEAD < n_units
                 if ahead:
                     stage_max(n + LEAD, 0)
-                stage_product(n, 0)
+                product_gpsimd(n)
+                product_vector(n, 0)
                 if ahead:
                     stage_max(n + LEAD, 1)
                     stage_copy(n + LEAD)
-                stage_product(n, 1)
+                product_vector(n, 1)
                 if n + 2 < n_units:
                     stage_sub(n + 2)
                 if ahead and units[n + LEAD][1][-1] == KK - 1:
                     merge_max(units[n + LEAD][0])
-                if ons is not None:
-                    ons = finish_vector(c - 1)
+                if back == 1:
+                    rz = reciprocal_z(tb)
+                elif back in (2, 3):
+                    scale_pair(c - 1, back - 2, tb, rz, sums[3])
                 if taps[-1] == KK - 1 and c + 1 < NCH:
                     load_windows(c + 1)
                 stage_add(n)
-                if ons is not None:
-                    finish_store(c - 1, ons)
-                    ons = None
-                if taps[-1] == KK - 1:
-                    ons = []
-            finish_store(NCH - 1, finish_vector(NCH - 1))
+                if n < len(late_steps):
+                    for step in late_steps[n]:
+                        step()
+            sums = empty_sums(NCH - 1)
+            rz = reciprocal_z(turn_back(sums[0]))
+            for i in range(2):
+                scale_pair(NCH - 1, i, turn_back(sums[1 + i]), rz, sums[3])

@@ -86,10 +86,10 @@ def tile_involution_kernel(tc, x, w_reduce, b_reduce, w_span, b_span, out):
                 stop=True,
             )
 
-        def stage_pass(u):
+        def stage_pass(u, times=1):
             c, taps = units[u]
             ps = psum.tile([P, 512], F32, tag="mm", name="ps")
-            for k, t in enumerate(taps):
+            for k, t in list(enumerate(taps)) * times:
                 nc.tensor.matmul_mx(
                     out=ps[:, k * CHQ : (k + 1) * CHQ],
                     lhsT=ws_codes[:, t * P : (t + 1) * P].bitcast(FP8X4),
@@ -524,8 +524,7 @@ def tile_involution_kernel(tc, x, w_reduce, b_reduce, w_span, b_span, out):
             for n in range(n_units):
                 c, taps = units[n]
                 back = n % upc if c > 0 else upc
-                if n + LEAD + 1 < n_units:
-                    stage_pass(n + LEAD + 1)
+                stage_pass(n + LEAD + 1 if n + LEAD + 1 < n_units else n_units - 2, 2)
                 if n + 2 < n_units and units[n + 2][1][0] == 0:
                     max_to_psum(units[n + 2][0])
                 if back == 1:

@@ -29,7 +29,6 @@ CHR = H // NCH
 CHQ = CHR * W
 QB = CHQ // P
 WS_TAPS = 8
-NCOPY = 8
 XROWS = HP * W
 XK = W + PAD
 XL = 1352
@@ -46,19 +45,17 @@ def tile_involution_kernel(tc, x, w_reduce, b_reduce, w_span, b_span, out):
         pacc = ctx.enter_context(tc.psum_pool(name="pacc", bufs=1))
 
         out_v = out[0].rearrange("(g j) h w -> g j (h w)", j=CC)
-        pairs = []
-        for i in range(0, K7, 2):
-            rows = range(i, min(i + 2, K7))
-            pairs += [[r * K7 + j, r * K7 + j + 1] for r in rows for j in range(0, K7 - 1, 2)]
-            pairs.append([r * K7 + K7 - 1 for r in rows])
-        upc = len(pairs)
-        units = [(c, taps) for c in range(NCH) for taps in pairs]
+        halves = [[i * K7 + j for j in js] for i in range(K7) for js in (range(4), range(4, K7))]
+        upc = len(halves)
+        units = [(c, taps) for c in range(NCH) for taps in halves]
         n_units = len(units)
         LEAD = upc + 2
         ps_of = {}
         kb_of = {}
         e_of = {}
         pr_of = {}
+        nv_of = {}
+        osb_of = {}
         acc_of = {}
         xw_of = {}
         mm_of = {}
@@ -78,6 +75,8 @@ def tile_involution_kernel(tc, x, w_reduce, b_reduce, w_span, b_span, out):
                     stop=True,
                 )
             xw_of[c] = xw0
+            if c < NCH - 1:
+                return
             nc.tensor.matmul(
                 out=xw2,
                 lhsT=ident_bf[:],
@@ -86,42 +85,44 @@ def tile_involution_kernel(tc, x, w_reduce, b_reduce, w_span, b_span, out):
                 stop=True,
             )
 
-        def stage_pass(u, times=1):
+        def stage_pass(u):
             c, taps = units[u]
-            ps = psum.tile([P, 512], F32, tag="mm", name="ps")
-            for k, t in list(enumerate(taps)) * times:
-                nc.tensor.matmul_mx(
-                    out=ps[:, k * CHQ : (k + 1) * CHQ],
-                    lhsT=ws_codes[:, t * P : (t + 1) * P].bitcast(FP8X4),
-                    lhsT_scale=ws_scl[:, t * P : (t + 1) * P],
-                    rhs=red_codes[:, c * CHQ : (c + 1) * CHQ].bitcast(FP8X4),
-                    rhs_scale=red_scl[:, c * CHQ : (c + 1) * CHQ],
-                    start=True,
-                    stop=True,
-                )
-            ps_of[u] = ps
+            ps_of[u] = []
+            for k0 in range(0, len(taps), 2):
+                ps = psum.tile([P, 512], F32, tag="mm", name="ps")
+                for k, t in enumerate(taps[k0 : k0 + 2]):
+                    nc.tensor.matmul_mx(
+                        out=ps[:, k * CHQ : (k + 1) * CHQ],
+                        lhsT=ws_codes[:, t * P : (t + 1) * P].bitcast(FP8X4),
+                        lhsT_scale=ws_scl[:, t * P : (t + 1) * P],
+                        rhs=red_codes[:, c * CHQ : (c + 1) * CHQ].bitcast(FP8X4),
+                        rhs_scale=red_scl[:, c * CHQ : (c + 1) * CHQ],
+                        start=True,
+                        stop=True,
+                    )
+                ps_of[u].append(ps)
 
         def stage_max(u, k):
             c, taps = units[u]
             if k >= len(taps):
                 return
             t = taps[k]
-            if u % upc == 0 and k == 0:
+            if t == 0:
                 mm_of[c] = stage.tile([P, 512], F32, name="mm", bufs=2)
-            mk = mm_of[c][:, k * CHQ : (k + 1) * CHQ]
-            pk = ps_of[u][:, k * CHQ : (k + 1) * CHQ]
-            if u % upc == 0:
+            mk = mm_of[c][:, k % 2 * CHQ : (k % 2 + 1) * CHQ]
+            pk = ps_of[u][k // 2][:, k % 2 * CHQ : (k % 2 + 1) * CHQ]
+            if t < 2:
                 nc.vector.tensor_scalar_add(out=mk, in0=pk, scalar1=bs[:, t : t + 1])
             else:
                 nc.vector.scalar_tensor_tensor(
                     out=mk, in0=pk, scalar=bs[:, t : t + 1], in1=mk, op0=ALU.add, op1=ALU.max
                 )
 
-        def stage_copy(u):
-            n = len(units[u][1]) * CHQ
-            kb = stage.tile([P, 512], F32, name="kb", bufs=LEAD + 2)
-            nc.scalar.copy(out=kb[:, 0:n], in_=ps_of[u][:, 0:n])
-            kb_of[u] = kb
+        def stage_copy(u, b):
+            n = min(2, len(units[u][1]) - 2 * b) * CHQ
+            if b == 0:
+                kb_of[u] = stage.tile([P, 4 * CHQ], F32, name="kb", bufs=LEAD + 1)
+            nc.scalar.copy(out=kb_of[u][:, 2 * b * CHQ : 2 * b * CHQ + n], in_=ps_of[u][b][:, 0:n])
 
         def merge_max(c):
             ms = stage.tile([P, CHQ], F32, name="ms", bufs=2)
@@ -144,7 +145,7 @@ def tile_involution_kernel(tc, x, w_reduce, b_reduce, w_span, b_span, out):
 
         def stage_exp(u):
             c, taps = units[u]
-            e = main.tile([P, 512], F32, name="e", bufs=4)
+            e = main.tile([P, 4 * CHQ], F32, name="e", bufs=4)
             for k, t in enumerate(taps):
                 nc.scalar.activation(
                     out=e[:, k * CHQ : (k + 1) * CHQ],
@@ -156,14 +157,14 @@ def tile_involution_kernel(tc, x, w_reduce, b_reduce, w_span, b_span, out):
             e_of[u] = e
 
         def vector_has_channel_2(u):
-            return u % 5 == 4
+            return u > n_units - upc and u % 2 == 0
 
         def product_gpsimd(u):
             c, taps = units[u]
             n = len(taps)
             j0 = 1 if vector_has_channel_2(u) else 0
             ng = 2 - j0
-            pg = main.tile([P, 4 * CHQ], F32, name="pg", bufs=4)
+            pg = main.tile([P, 8 * CHQ], F32, name="pg", bufs=3)
             s0 = taps[0] % K7
             q0 = (taps[0] // K7 + c * CHR) * W
             nc.gpsimd.tensor_tensor(
@@ -172,10 +173,11 @@ def tile_involution_kernel(tc, x, w_reduce, b_reduce, w_span, b_span, out):
                 .rearrange("p (k q) -> p k q", k=n)
                 .unsqueeze(2)
                 .to_broadcast([P, n, ng, CHQ]),
-                in1=xs[:].rearrange("p (s j q) -> p s j q", s=NCOPY, j=2)[:, s0 : s0 + n, j0:2, q0 : q0 + CHQ],
+                in1=xs[:].rearrange("p (s j q) -> p s j q", s=K7, j=2)[:, s0 : s0 + n, j0:2, q0 : q0 + CHQ],
                 op=ALU.mult,
             )
             pr_of[u] = [[pg[:, (k * ng * QB + i) * P : (k * ng * QB + i + 1) * P] for i in range(ng * QB)] for k in range(n)]
+            nv_of[u] = 4 - ng
 
         def product_vector(u, k):
             c, taps = units[u]
@@ -183,7 +185,7 @@ def tile_involution_kernel(tc, x, w_reduce, b_reduce, w_span, b_span, out):
                 return
             off = (taps[k] // K7) * XK + taps[k] % K7
             ek3 = e_of[u][:, k * CHQ : (k + 1) * CHQ].rearrange("p (h w) -> p h w", w=W)
-            pv = main.tile([P, 2 * CHQ], F32, name="pv", bufs=6)
+            pv = main.tile([P, 2 * CHQ], F32, name="pv", bufs=10)
             nc.vector.tensor_tensor(
                 out=pv[:].rearrange("p (j h w) -> p j h w", j=2, w=W),
                 in0=xw_of[c][:]
@@ -194,7 +196,7 @@ def tile_involution_kernel(tc, x, w_reduce, b_reduce, w_span, b_span, out):
             )
             blocks = [pv[:, i * P : (i + 1) * P] for i in range(2 * QB)]
             if vector_has_channel_2(u):
-                pv2 = main.tile([P, CHQ], F32, name="pv2", bufs=4)
+                pv2 = main.tile([P, CHQ], F32, tag="pv", name="pv2", bufs=10)
                 nc.vector.tensor_tensor(
                     out=pv2[:].rearrange("p (h w) -> p h w", w=W),
                     in0=xw2[:, off : off + XWIN].rearrange("p (h k) -> p h k", k=XK)[:, :, 0:W],
@@ -214,34 +216,37 @@ def tile_involution_kernel(tc, x, w_reduce, b_reduce, w_span, b_span, out):
                 is_transpose=True,
             )
 
-        def stage_add(u):
+        def add_tap(u, k, of_vector):
             c, taps = units[u]
-            if u % upc == 0:
-                acc_of[c] = [pacc.tile([P, 512], F32, tag="acc%d" % i, name="acc") for i in range(3)]
-            accz, acc_a, acc_b = acc_of[c]
-            for k, t in enumerate(taps):
-                blocks = pr_of[u][k]
-                first = t == 0
-                last = t == KK - 1
+            if k >= len(taps):
+                return
+            t = taps[k]
+            first = t == 0
+            last = t == KK - 1
+            if first:
+                acc_of.setdefault(c, [])
+                for i in (0, 1) if of_vector else (2,):
+                    acc_of[c].append(pacc.tile([P, 512], F32, tag="acc%d" % i, name="acc"))
+            if of_vector:
                 for qb in range(QB):
                     q0 = k * CHQ + qb * P
-                    add_block(accz, qb, e_of[u][:, q0 : q0 + P], first and qb == 0, last and qb == QB - 1)
-                for b, bank in enumerate((acc_a, acc_b)):
-                    for i in range(2 * QB):
-                        add_block(bank, i, blocks[2 * QB * b + i], first and i == 0, last and i == 2 * QB - 1)
+                    add_block(acc_of[c][0], qb, e_of[u][:, q0 : q0 + P], first and qb == 0, last and qb == QB - 1)
+            n_vector = nv_of[u] * QB
+            for i in range(n_vector) if of_vector else range(n_vector, CC * QB):
+                slot = i % (2 * QB)
+                add_block(
+                    acc_of[c][1 + i // (2 * QB)], slot, pr_of[u][k][i], first and slot == 0, last and slot == 2 * QB - 1
+                )
 
-        def empty_sums(c):
-            accz, acc_a, acc_b = acc_of[c]
+        def empty_z_and_a(c):
             zs = main.tile([P, CHQ], F32, name="zs", bufs=1)
-            nc.scalar.copy(out=zs[:], in_=accz[:, 0:CHQ])
-            sums = [zs]
-            for bank in (acc_a, acc_b):
-                sm = main.tile([P, 512], F32, name="sm", bufs=2)
-                nc.scalar.copy(out=sm[:], in_=bank[:])
-                sums.append(sm)
-            osb = main.tile([P, CC * CHQ], F32, name="osb", bufs=2)
-            sums.append(osb)
-            return sums
+            nc.scalar.copy(out=zs[:], in_=acc_of[c][0][:, 0:CHQ])
+            sums = const.tile([P, 1024], F32, tag="xh1", name="sums")
+            nc.scalar.copy(out=sums[:, 0:512], in_=acc_of[c][1][:])
+            return zs, sums
+
+        def empty_b(c, sums):
+            nc.scalar.copy(out=sums[:, 512:1024], in_=acc_of[c][2][:])
 
         def turn_back(block):
             tb = psum.tile([P, 512], F32, tag="mm", name="tb")
@@ -254,7 +259,10 @@ def tile_involution_kernel(tc, x, w_reduce, b_reduce, w_span, b_span, out):
             nc.vector.reciprocal(out=rz[:], in_=tb[:, 0:CHQ])
             return rz
 
-        def scale_pair(c, i, tb, rz, osb):
+        def scale_pair(c, i, tb, rz):
+            if i == 0:
+                osb_of[c] = const.tile([P, CC * CHQ], F32, tag="xh0", name="osb")
+            osb = osb_of[c]
             nc.vector.tensor_tensor(
                 out=osb[:, i * 512 : (i + 1) * 512].rearrange("p (j n) -> p j n", j=2),
                 in0=tb[:].rearrange("p (j n) -> p j n", j=2),
@@ -268,9 +276,10 @@ def tile_involution_kernel(tc, x, w_reduce, b_reduce, w_span, b_span, out):
 
         def stage_kern(u):
             stage_pass(u)
-            stage_max(u, 0)
-            stage_max(u, 1)
-            stage_copy(u)
+            for b in range(2):
+                stage_max(u, 2 * b)
+                stage_max(u, 2 * b + 1)
+                stage_copy(u, b)
 
         with tc.tile_pool(name="head", bufs=1) as head:
             ident = const.tile([P, P], F32)
@@ -279,14 +288,14 @@ def tile_involution_kernel(tc, x, w_reduce, b_reduce, w_span, b_span, out):
             make_identity(nc, ident_bf[:])
 
             wr_sb = head.tile([P, 4 * 512], BF16)
-            x_half = [const.tile([P, CC * 512], BF16, name="xh%d" % i) for i in range(2)]
+            x_half = [const.tile([P, CC * 512], BF16, tag="xh%d" % i, name="xh") for i in range(2)]
             br_b = const.tile([P, 4], BF16)
             bs_b = const.tile([P, KK], BF16)
             br = const.tile([P, 4], F32)
             bs = const.tile([P, KK], F32)
             xp = const.tile([P, 3 * XL], BF16)
-            xs = const.tile([P, NCOPY * 2 * XROWS], BF16)
-            xs5 = xs[:].rearrange("p (s j h w) -> p s j h w", s=NCOPY, j=2, w=W)
+            xs = const.tile([P, K7 * 2 * XROWS], BF16)
+            xs5 = xs[:].rearrange("p (s j h w) -> p s j h w", s=K7, j=2, w=W)
             gw = head.tile([P, 4 * P * 4], BF16, align_bytes=64)
             wr_codes = const.tile([P, 4 * P], U32, align_bytes=64)
             wr_scl = const.tile([P, 4 * P], U8, align_bytes=64)
@@ -331,23 +340,23 @@ def tile_involution_kernel(tc, x, w_reduce, b_reduce, w_span, b_span, out):
                 )
 
             def zero_xs_rows():
-                for rows in (slice(0, PAD), slice(HP - PAD - 1, HP)):
+                for rows in (slice(0, PAD), slice(HP - PAD, HP)):
                     nc.gpsimd.memset(
                         xs[:].rearrange("p (n h w) -> p n (h w)", h=HP, w=W)[:, :, rows.start * W : rows.stop * W], 0.0
                     )
 
             def zero_xs_columns():
-                for s in range(NCOPY):
-                    d = min(s, K7 - 1) - PAD
+                for s in range(K7):
+                    d = s - PAD
                     if d != 0:
                         cols = slice(0, 4) if d < 0 else slice(W - 4, W)
-                        nc.vector.memset(xs5[:, s, :, PAD : HP - PAD - 1, cols], 0.0)
+                        nc.vector.memset(xs5[:, s, :, PAD : HP - PAD, cols], 0.0)
 
             def xs_views(s, h0, h1):
                 i = h0 // (H // 2)
-                d = min(s, K7 - 1) - PAD
+                d = s - PAD
                 w0, w1 = max(0, -d), min(W, W - d)
-                r0 = h0 + PAD - s // K7
+                r0 = h0 + PAD
                 src = x_half[i][:].rearrange("p (j h w) -> p j h w", j=CC, w=W)
                 b = i * (H // 2)
                 return xs5[:, s, :, r0 : r0 + h1 - h0, w0:w1], src[:, 2:4, h0 - b : h1 - b, w0 + d : w1 + d]
@@ -375,7 +384,7 @@ def tile_involution_kernel(tc, x, w_reduce, b_reduce, w_span, b_span, out):
 
             def group_part(key, src, engine_copy, q0, q1):
                 if key not in groups:
-                    groups[key] = const.tile([P, 4 * 512], BF16, tag="grp", name="grp", bufs=2, align_bytes=64)
+                    groups[key] = const.tile([P, 4 * 512], BF16, tag="grp", name="grp", bufs=1, align_bytes=64)
                 engine_copy(
                     out=groups[key][:].rearrange("p (q j) -> p q j", j=4)[:, q0:q1, :],
                     in_=src.rearrange("p (j q) -> p q j", j=4)[:, q0:q1, :],
@@ -390,7 +399,7 @@ def tile_involution_kernel(tc, x, w_reduce, b_reduce, w_span, b_span, out):
 
             def red_pass(i, a, on_vector):
                 if a == 0:
-                    red_of[i] = const.tile([P, 4 * 512], BF16, name="red", bufs=2)
+                    red_of[i] = const.tile([P, 4 * 512], BF16, name="red", bufs=1)
                 ps = psum.tile([P, 512], F32, tag="mm", name="ps")
                 nc.tensor.matmul_mx(
                     out=ps[:],
@@ -426,7 +435,7 @@ def tile_involution_kernel(tc, x, w_reduce, b_reduce, w_span, b_span, out):
                                 ws32[:, 4 * g % WS_TAPS + 2 * b + tl, u, :],
                                 ident[:],
                             )
-                    copy = nc.vector.tensor_copy if b == 1 and g % 3 != 0 else nc.scalar.copy
+                    copy = nc.vector.tensor_copy if b == 1 and g % 6 == 5 else nc.scalar.copy
                     copy(
                         out=gws32[:, 2 * b : 2 * b + nb, :, :],
                         in_=tp[:].rearrange("p (t u g) -> p t g u", t=2, u=2)[:, 0:nb, :, :],
@@ -469,7 +478,7 @@ def tile_involution_kernel(tc, x, w_reduce, b_reduce, w_span, b_span, out):
                 nc.scalar.activation(out=warm[:], in_=br[:, 0:1], func=ACT.Exp, scale=1.0)
                 fill_xp(0)
                 fill_xp(1)
-                for s in range(NCOPY):
+                for s in range(K7):
                     fill_xs_gpsimd(s, 0, CHR + PAD)
 
                 turn_wr(0)
@@ -500,16 +509,18 @@ def tile_involution_kernel(tc, x, w_reduce, b_reduce, w_span, b_span, out):
                 merge_max(0)
 
             late_steps = [
-                [lambda q0=q0: group_part("x1", x_half[1][:], nc.scalar.copy, q0, q0 + 256)] for q0 in (0, 256)
+                [lambda: group_part("x1", x_half[1][:], nc.scalar.copy, 0, 512)],
+                [lambda: quantise_half(x_codes, x_scl, 1, groups["x1"])],
+                [lambda: red_pass(1, 0, False)],
+                [lambda: red_pass(1, 1, False)],
+                [lambda: red_pass(1, 2, False)],
+                [lambda: red_pass(1, 3, False)],
+                [lambda: group_part("r1", red_of[1][:], nc.scalar.copy, 0, 512)],
+                [lambda: quantise_half(red_codes, red_scl, 1, groups["r1"])],
             ]
-            late_steps.append([lambda: quantise_half(x_codes, x_scl, 1, groups["x1"])])
-            late_steps += [[lambda a=a: red_pass(1, a, False)] for a in range(4)]
             late_steps += [
-                [lambda q0=q0: group_part("r1", red_of[1][:], nc.scalar.copy, q0, q0 + 256)] for q0 in (0, 256)
-            ]
-            late_steps.append([lambda: quantise_half(red_codes, red_scl, 1, groups["r1"])])
-            late_steps += [
-                [lambda s=s, h=h: fill_xs_scalar(s, *h) for h in ((CHR + PAD, H // 2), (H // 2, H))] for s in range(NCOPY)
+                [lambda s=s, h=h: fill_xs_scalar(s, *h) for s in ss for h in ((CHR + PAD, H // 2), (H // 2, H))]
+                for ss in ((0, 1), (2, 3), (4, 5), (6,))
             ]
         main = ctx.enter_context(tc.tile_pool(name="main", bufs=1))
 
@@ -523,42 +534,56 @@ def tile_involution_kernel(tc, x, w_reduce, b_reduce, w_span, b_span, out):
             stage_pass(LEAD)
             for n in range(n_units):
                 c, taps = units[n]
+                last_k = len(taps) - 1
+                ends = n % upc == upc - 1
                 back = n % upc if c > 0 else upc
-                stage_pass(n + LEAD + 1 if n + LEAD + 1 < n_units else n_units - 2, 2)
-                if n + 2 < n_units and units[n + 2][1][0] == 0:
-                    max_to_psum(units[n + 2][0])
+                ahead = n + LEAD < n_units
                 if back == 1:
-                    tb = turn_back(sums[0])
+                    tb = turn_back(zs)
                 elif back in (2, 3):
-                    tb = turn_back(sums[back - 1])
+                    tb = turn_back(sums[:, (back - 2) * 512 : (back - 1) * 512])
                 if n + 1 < n_units:
                     stage_exp(n + 1)
                 if back == 0:
-                    sums = empty_sums(c - 1)
-                ahead = n + LEAD < n_units
-                if ahead:
-                    stage_max(n + LEAD, 0)
+                    zs, sums = empty_z_and_a(c - 1)
+                elif back == 1:
+                    empty_b(c - 1, sums)
                 product_gpsimd(n)
-                product_vector(n, 0)
-                if ahead:
-                    stage_max(n + LEAD, 1)
-                    stage_copy(n + LEAD)
-                product_vector(n, 1)
-                if n + 2 < n_units:
-                    stage_sub(n + 2)
-                if ahead and units[n + LEAD][1][-1] == KK - 1:
-                    merge_max(units[n + LEAD][0])
+                for k in range(4):
+                    product_vector(n, k)
+                    if k == 0 and n + 2 < n_units:
+                        stage_sub(n + 2)
+                    if ahead and k == 1:
+                        stage_max(n + LEAD, 0)
+                        stage_max(n + LEAD, 1)
+                        stage_copy(n + LEAD, 0)
+                    if ahead and k == 2:
+                        stage_max(n + LEAD, 2)
+                    if ahead and k == 3:
+                        stage_max(n + LEAD, 3)
+                        stage_copy(n + LEAD, 1)
+                    if k == last_k and ends and c + 1 < NCH:
+                        load_windows(c + 1)
+                    add_tap(n, k, True)
                 if back == 1:
                     rz = reciprocal_z(tb)
                 elif back in (2, 3):
-                    scale_pair(c - 1, back - 2, tb, rz, sums[3])
-                if taps[-1] == KK - 1 and c + 1 < NCH:
-                    load_windows(c + 1)
-                stage_add(n)
+                    scale_pair(c - 1, back - 2, tb, rz)
+                if n + LEAD + 1 < n_units:
+                    stage_pass(n + LEAD + 1)
+                if ahead and (n + LEAD) % upc == upc - 1:
+                    merge_max((n + LEAD) // upc)
+                    max_to_psum((n + LEAD) // upc)
+                if n > 0:
+                    for k in range(4):
+                        add_tap(n - 1, k, False)
                 if n < len(late_steps):
                     for step in late_steps[n]:
                         step()
-            sums = empty_sums(NCH - 1)
-            rz = reciprocal_z(turn_back(sums[0]))
-            for i in range(2):
-                scale_pair(NCH - 1, i, turn_back(sums[1 + i]), rz, sums[3])
+            zs, sums = empty_z_and_a(NCH - 1)
+            rz = reciprocal_z(turn_back(zs))
+            for k in range(4):
+                add_tap(n_units - 1, k, False)
+            scale_pair(NCH - 1, 0, turn_back(sums[:, 0:512]), rz)
+            empty_b(NCH - 1, sums)
+            scale_pair(NCH - 1, 1, turn_back(sums[:, 512:1024]), rz)

@@ -56,6 +56,7 @@ def tile_involution_kernel(tc, x, w_reduce, b_reduce, w_span, b_span, out):
         pr_of = {}
         nv_of = {}
         osb_of = {}
+        z_of = {}
         acc_of = {}
         xw_of = {}
         mm_of = {}
@@ -90,7 +91,7 @@ def tile_involution_kernel(tc, x, w_reduce, b_reduce, w_span, b_span, out):
             ps_of[u] = []
             for k0 in range(0, len(taps), 2):
                 ps = psum.tile([P, 512], F32, tag="mm", name="ps")
-                for k, t in enumerate(taps[k0 : k0 + 2]):
+                for k, t in enumerate(taps[k0 : k0 + 2]) if k0 + 1 < len(taps) else [(0, taps[k0])] * 2:
                     nc.tensor.matmul_mx(
                         out=ps[:, k * CHQ : (k + 1) * CHQ],
                         lhsT=ws_codes[:, t * P : (t + 1) * P].bitcast(FP8X4),
@@ -157,7 +158,7 @@ def tile_involution_kernel(tc, x, w_reduce, b_reduce, w_span, b_span, out):
             e_of[u] = e
 
         def vector_has_channel_2(u):
-            return u > n_units - upc and u % 2 == 0
+            return u >= n_units - upc and u % upc in (4, 6, 8, 10)
 
         def product_gpsimd(u):
             c, taps = units[u]
@@ -216,6 +217,19 @@ def tile_involution_kernel(tc, x, w_reduce, b_reduce, w_span, b_span, out):
                 is_transpose=True,
             )
 
+        def add_z(u, k):
+            c, taps = units[u]
+            if k >= len(taps):
+                return
+            t = taps[k]
+            if t == 0:
+                z_of[c] = pacc.tile([P, 512], F32, tag="acc0", name="acc")
+            for qb in range(QB):
+                q0 = k * CHQ + qb * P
+                add_block(
+                    z_of[c], qb, e_of[u][:, q0 : q0 + P], t == 0 and qb == 0, t == KK - 1 and qb == QB - 1
+                )
+
         def add_tap(u, k, of_vector):
             c, taps = units[u]
             if k >= len(taps):
@@ -225,28 +239,26 @@ def tile_involution_kernel(tc, x, w_reduce, b_reduce, w_span, b_span, out):
             last = t == KK - 1
             if first:
                 acc_of.setdefault(c, [])
-                for i in (0, 1) if of_vector else (2,):
-                    acc_of[c].append(pacc.tile([P, 512], F32, tag="acc%d" % i, name="acc"))
-            if of_vector:
-                for qb in range(QB):
-                    q0 = k * CHQ + qb * P
-                    add_block(acc_of[c][0], qb, e_of[u][:, q0 : q0 + P], first and qb == 0, last and qb == QB - 1)
+                acc_of[c].append(pacc.tile([P, 512], F32, tag="acc%d" % (1 if of_vector else 2), name="acc"))
             n_vector = nv_of[u] * QB
             for i in range(n_vector) if of_vector else range(n_vector, CC * QB):
                 slot = i % (2 * QB)
                 add_block(
-                    acc_of[c][1 + i // (2 * QB)], slot, pr_of[u][k][i], first and slot == 0, last and slot == 2 * QB - 1
+                    acc_of[c][i // (2 * QB)], slot, pr_of[u][k][i], first and slot == 0, last and slot == 2 * QB - 1
                 )
 
-        def empty_z_and_a(c):
+        def empty_z(c):
             zs = main.tile([P, CHQ], F32, name="zs", bufs=1)
-            nc.scalar.copy(out=zs[:], in_=acc_of[c][0][:, 0:CHQ])
+            nc.scalar.copy(out=zs[:], in_=z_of[c][:, 0:CHQ])
+            return zs
+
+        def empty_a(c):
             sums = const.tile([P, 1024], F32, tag="xh1", name="sums")
-            nc.scalar.copy(out=sums[:, 0:512], in_=acc_of[c][1][:])
-            return zs, sums
+            nc.scalar.copy(out=sums[:, 0:512], in_=acc_of[c][0][:])
+            return sums
 
         def empty_b(c, sums):
-            nc.scalar.copy(out=sums[:, 512:1024], in_=acc_of[c][2][:])
+            nc.scalar.copy(out=sums[:, 512:1024], in_=acc_of[c][1][:])
 
         def turn_back(block):
             tb = psum.tile([P, 512], F32, tag="mm", name="tb")
@@ -312,9 +324,10 @@ def tile_involution_kernel(tc, x, w_reduce, b_reduce, w_span, b_span, out):
             x_view = x[0].rearrange("(g j) h w -> g j (h w)", j=CC)
             ws_view = w_span.rearrange("(g t) r -> g t r", t=KK)
 
-            def load_x(i):
+            def load_x(i, q0, q1):
                 nc.sync.dma_start(
-                    out=x_half[i][:].rearrange("p (j q) -> p j q", j=CC), in_=x_view[:, :, i * 512 : (i + 1) * 512]
+                    out=x_half[i][:].rearrange("p (j q) -> p j q", j=CC)[:, :, q0:q1],
+                    in_=x_view[:, :, i * 512 + q0 : i * 512 + q1],
                 )
 
             def load_ws(a):
@@ -382,41 +395,51 @@ def tile_involution_kernel(tc, x, w_reduce, b_reduce, w_span, b_span, out):
                     out=gw32[:, 2 * b : 2 * b + 2, :, :], in_=tp[:].rearrange("p (a v r) -> p a r v", a=2, v=2)
                 )
 
-            def group_part(key, src, engine_copy, q0, q1):
-                if key not in groups:
-                    groups[key] = const.tile([P, 4 * 512], BF16, tag="grp", name="grp", bufs=1, align_bytes=64)
+            def group(key, src, engine_copy):
+                groups[key] = const.tile([P, 4 * CHQ], BF16, tag="grp", name="grp", bufs=2, align_bytes=64)
                 engine_copy(
-                    out=groups[key][:].rearrange("p (q j) -> p q j", j=4)[:, q0:q1, :],
-                    in_=src.rearrange("p (j q) -> p q j", j=4)[:, q0:q1, :],
+                    out=groups[key][:].rearrange("p (q j) -> p q j", j=4), in_=src.rearrange("p j q -> p q j")
                 )
 
-            def quantise_half(codes, scl, i, grouped):
+            def group_x(c, engine_copy):
+                q0 = c % 2 * CHQ
+                group(("x", c), x_half[c // 2][:].rearrange("p (j q) -> p j q", j=CC)[:, :, q0 : q0 + CHQ], engine_copy)
+
+            def group_red(c, engine_copy):
+                group(("red", c), red_of[c][:].rearrange("p (a q) -> p a q", a=4), engine_copy)
+
+            def quantise_chunk(codes, scl, c, key):
                 nc.vector.quantize_mx(
-                    out=codes[:, i * 512 : (i + 1) * 512].bitcast(FP8X4),
-                    scales=scl[:, i * 512 : (i + 1) * 512],
-                    in_=grouped[:],
+                    out=codes[:, c * CHQ : (c + 1) * CHQ].bitcast(FP8X4),
+                    scales=scl[:, c * CHQ : (c + 1) * CHQ],
+                    in_=groups[key, c][:],
                 )
 
-            def red_pass(i, a, on_vector):
-                if a == 0:
-                    red_of[i] = const.tile([P, 4 * 512], BF16, name="red", bufs=1)
+            def red_passes(c, a0, shared):
+                if a0 == 0:
+                    red_of[c] = const.tile([P, 4 * CHQ], BF16, tag="red", name="red", bufs=2)
                 ps = psum.tile([P, 512], F32, tag="mm", name="ps")
-                nc.tensor.matmul_mx(
-                    out=ps[:],
-                    lhsT=wr_codes[:, a * P : (a + 1) * P].bitcast(FP8X4),
-                    lhsT_scale=wr_scl[:, a * P : (a + 1) * P],
-                    rhs=x_codes[:, i * 512 : (i + 1) * 512].bitcast(FP8X4),
-                    rhs_scale=x_scl[:, i * 512 : (i + 1) * 512],
-                    start=True,
-                    stop=True,
-                )
-                dst = red_of[i][:, a * 512 : (a + 1) * 512]
-                if on_vector:
-                    nc.vector.tensor_scalar(
-                        out=dst, in0=ps[:], scalar1=br[:, a : a + 1], scalar2=0.0, op0=ALU.add, op1=ALU.max
+                for i in range(2):
+                    a = a0 + i
+                    nc.tensor.matmul_mx(
+                        out=ps[:, i * CHQ : (i + 1) * CHQ],
+                        lhsT=wr_codes[:, a * P : (a + 1) * P].bitcast(FP8X4),
+                        lhsT_scale=wr_scl[:, a * P : (a + 1) * P],
+                        rhs=x_codes[:, c * CHQ : (c + 1) * CHQ].bitcast(FP8X4),
+                        rhs_scale=x_scl[:, c * CHQ : (c + 1) * CHQ],
+                        start=True,
+                        stop=True,
                     )
-                else:
-                    nc.scalar.activation(out=dst, in_=ps[:], func=ACT.Relu, bias=br[:, a : a + 1], scale=1.0)
+                for i in range(2):
+                    a = a0 + i
+                    dst = red_of[c][:, a * CHQ : (a + 1) * CHQ]
+                    src = ps[:, i * CHQ : (i + 1) * CHQ]
+                    if shared and a0 == 2:
+                        nc.vector.tensor_scalar(
+                            out=dst, in0=src, scalar1=br[:, a : a + 1], scalar2=0.0, op0=ALU.add, op1=ALU.max
+                        )
+                    else:
+                        nc.scalar.activation(out=dst, in_=src, func=ACT.Relu, bias=br[:, a : a + 1], scale=1.0)
 
             n_groups = (KK + 3) // 4
 
@@ -457,7 +480,7 @@ def tile_involution_kernel(tc, x, w_reduce, b_reduce, w_span, b_span, out):
                     out=wr_sb[:].rearrange("p (u f) -> p u f", u=2),
                     in_=w_reduce.rearrange("(u p e) c -> p u (e c)", u=2, e=2),
                 )
-                load_x(0)
+                load_x(0, 0, CHQ)
                 with nc.allow_non_contiguous_dma(reason="two small bias vectors"):
                     nc.sync.dma_start(
                         out=br_b[:].rearrange("p (u e) -> p u e", u=2),
@@ -465,8 +488,9 @@ def tile_involution_kernel(tc, x, w_reduce, b_reduce, w_span, b_span, out):
                     )
                     load_ws(0)
                     nc.sync.dma_start(out=bs_b[:], in_=b_span.rearrange("(g t) -> g t", t=KK))
+                load_x(0, CHQ, 512)
                 load_ws(1)
-                load_x(1)
+                load_x(1, 0, 512)
                 load_ws(2)
                 load_ws(3)
 
@@ -483,18 +507,18 @@ def tile_involution_kernel(tc, x, w_reduce, b_reduce, w_span, b_span, out):
 
                 turn_wr(0)
                 turn_wr(1)
-                group_part("x0", x_half[0][:], nc.vector.tensor_copy, 0, 512)
+                group_x(0, nc.vector.tensor_copy)
                 nc.vector.tensor_copy(out=br[:], in_=br_b[:])
                 nc.vector.quantize_mx(out=wr_codes[:].bitcast(FP8X4), scales=wr_scl[:], in_=gw[:])
-                quantise_half(x_codes, x_scl, 0, groups["x0"])
-                for a in range(4):
-                    red_pass(0, a, a % 2 == 1)
+                quantise_chunk(x_codes, x_scl, 0, "x")
+                red_passes(0, 0, True)
+                red_passes(0, 2, True)
                 turn_ws(0)
                 nc.vector.tensor_copy(out=bs[:], in_=bs_b[:])
-                group_part("r0", red_of[0][:], nc.vector.tensor_copy, 0, 512)
+                group_red(0, nc.vector.tensor_copy)
                 turn_ws(1)
                 quantise_ws(0)
-                quantise_half(red_codes, red_scl, 0, groups["r0"])
+                quantise_chunk(red_codes, red_scl, 0, "red")
                 done = 0
                 for g in range(1, n_groups + 2):
                     if g + 1 < n_groups:
@@ -506,18 +530,25 @@ def tile_involution_kernel(tc, x, w_reduce, b_reduce, w_span, b_span, out):
                         done += 1
                     if g == 4:
                         load_windows(0)
+                    if g == 5:
+                        group_x(1, nc.vector.tensor_copy)
+                        quantise_chunk(x_codes, x_scl, 1, "x")
+                    if g in (6, 7):
+                        red_passes(1, 2 * g - 12, False)
+                    if g == 9:
+                        group_red(1, nc.vector.tensor_copy)
+                        quantise_chunk(red_codes, red_scl, 1, "red")
                 merge_max(0)
 
-            late_steps = [
-                [lambda: group_part("x1", x_half[1][:], nc.scalar.copy, 0, 512)],
-                [lambda: quantise_half(x_codes, x_scl, 1, groups["x1"])],
-                [lambda: red_pass(1, 0, False)],
-                [lambda: red_pass(1, 1, False)],
-                [lambda: red_pass(1, 2, False)],
-                [lambda: red_pass(1, 3, False)],
-                [lambda: group_part("r1", red_of[1][:], nc.scalar.copy, 0, 512)],
-                [lambda: quantise_half(red_codes, red_scl, 1, groups["r1"])],
-            ]
+            late_steps = []
+            for c in (2, 3):
+                late_steps += [
+                    [lambda c=c: group_x(c, nc.scalar.copy)],
+                    [lambda c=c: quantise_chunk(x_codes, x_scl, c, "x"), lambda c=c: red_passes(c, 0, False)],
+                    [lambda c=c: red_passes(c, 2, False)],
+                    [lambda c=c: group_red(c, nc.scalar.copy)],
+                    [lambda c=c: quantise_chunk(red_codes, red_scl, c, "red")],
+                ]
             late_steps += [
                 [lambda s=s, h=h: fill_xs_scalar(s, *h) for s in ss for h in ((CHR + PAD, H // 2), (H // 2, H))]
                 for ss in ((0, 1), (2, 3), (4, 5), (6,))
@@ -545,10 +576,16 @@ def tile_involution_kernel(tc, x, w_reduce, b_reduce, w_span, b_span, out):
                 if n + 1 < n_units:
                     stage_exp(n + 1)
                 if back == 0:
-                    zs, sums = empty_z_and_a(c - 1)
+                    zs = empty_z(c - 1)
+                    sums = empty_a(c - 1)
                 elif back == 1:
                     empty_b(c - 1, sums)
                 product_gpsimd(n)
+                if n == n_units - 1:
+                    for k in range(4):
+                        add_z(n, k)
+                    zs = empty_z(c)
+                    tb = turn_back(zs)
                 for k in range(4):
                     product_vector(n, k)
                     if k == 0 and n + 2 < n_units:
@@ -564,6 +601,8 @@ def tile_involution_kernel(tc, x, w_reduce, b_reduce, w_span, b_span, out):
                         stage_copy(n + LEAD, 1)
                     if k == last_k and ends and c + 1 < NCH:
                         load_windows(c + 1)
+                    if n < n_units - 1:
+                        add_z(n, k)
                     add_tap(n, k, True)
                 if back == 1:
                     rz = reciprocal_z(tb)
@@ -580,8 +619,8 @@ def tile_involution_kernel(tc, x, w_reduce, b_reduce, w_span, b_span, out):
                 if n < len(late_steps):
                     for step in late_steps[n]:
                         step()
-            zs, sums = empty_z_and_a(NCH - 1)
-            rz = reciprocal_z(turn_back(zs))
+            rz = reciprocal_z(tb)
+            sums = empty_a(NCH - 1)
             for k in range(4):
                 add_tap(n_units - 1, k, False)
             scale_pair(NCH - 1, 0, turn_back(sums[:, 0:512]), rz)

@@ -207,15 +207,20 @@ def tile_involution_kernel(tc, x, w_reduce, b_reduce, w_span, b_span, out):
                 blocks += [pv2[:, i * P : (i + 1) * P] for i in range(QB)]
             pr_of[u][k] = blocks + pr_of[u][k]
 
-        def add_block(bank, slot, block, first, last):
-            nc.tensor.matmul(
-                out=bank[:, slot * P : (slot + 1) * P],
-                lhsT=block,
-                rhs=ident[:],
-                start=first,
-                stop=last,
-                is_transpose=True,
-            )
+        def add_block(bank, slot, block, first, last, as_matmul=False):
+            if as_matmul:
+                nc.tensor.matmul(
+                    out=bank[:, slot * P : (slot + 1) * P], lhsT=block, rhs=ident[:], start=first, stop=last
+                )
+            else:
+                nc.tensor.matmul(
+                    out=bank[:, slot * P : (slot + 1) * P],
+                    lhsT=block,
+                    rhs=ident[:],
+                    start=first,
+                    stop=last,
+                    is_transpose=True,
+                )
 
         def add_z(u, k):
             c, taps = units[u]
@@ -244,7 +249,12 @@ def tile_involution_kernel(tc, x, w_reduce, b_reduce, w_span, b_span, out):
             for i in range(n_vector) if of_vector else range(n_vector, CC * QB):
                 slot = i % (2 * QB)
                 add_block(
-                    acc_of[c][i // (2 * QB)], slot, pr_of[u][k][i], first and slot == 0, last and slot == 2 * QB - 1
+                    acc_of[c][i // (2 * QB)],
+                    slot,
+                    pr_of[u][k][i],
+                    first and slot == 0,
+                    last and slot == 2 * QB - 1,
+                    as_matmul=of_vector and k == 0 and i in (2, 3),
                 )
 
         def empty_z(c):

from contextlib import ExitStack

import concourse.bass as bass
import concourse.mybir as mybir
import concourse.tile as tile
from concourse.masks import make_identity

F32 = mybir.dt.float32
BF16 = mybir.dt.bfloat16
U32 = mybir.dt.uint32
U8 = mybir.dt.uint8
FP8X4 = mybir.dt.float8_e4m3fn_x4
ALU = mybir.AluOpType
ACT = mybir.ActivationFunctionType

P = 128
CC = 4
H = 32
W = 32
HW = H * W
K7 = 7
KK = K7 * K7
PAD = 3
HP = H + 2 * PAD
WP = W + 2 * PAD
R = 512
NCH = 4
CHR = H // NCH
CHQ = CHR * W
QB = CHQ // P
WS_TAPS = 8
XROWS = HP * W
XK = W + PAD
XL = 1352
XWIN = CHR * XK
FLOPS = 2 * 512 * 512 * HW + 2 * KK * P * R * HW + 2 * KK * 512 * HW


def tile_involution_kernel(tc, x, w_reduce, b_reduce, w_span, b_span, out):
    nc = tc.nc
    with ExitStack() as ctx:
        const = ctx.enter_context(tc.tile_pool(name="const", bufs=1))
        stage = ctx.enter_context(tc.tile_pool(name="stage", bufs=3))
        psum = ctx.enter_context(tc.psum_pool(name="psum", bufs=3))
        pacc = ctx.enter_context(tc.psum_pool(name="pacc", bufs=1))

        out_v = out[0].rearrange("(g j) h w -> g j (h w)", j=CC)
        halves = [[i * K7 + j for j in js] for i in range(K7) for js in (range(4), range(4, K7))]
        upc = len(halves)
        units = [(c, taps) for c in range(NCH) for taps in halves]
        n_units = len(units)
        LEAD = upc + 2
        ps_of = {}
        kb_of = {}
        e_of = {}
        pr_of = {}
        nv_of = {}
        osb_of = {}
        z_of = {}
        acc_of = {}
        xw_of = {}
        mm_of = {}
        ms_of = {}
        side = pacc.tile([P, 512], F32, name="side")
        mp = side[:, 0:CHQ]
        xw2 = side[:, CHQ : 2 * CHQ].bitcast(BF16)

        def load_windows(c):
            xw0 = pacc.tile([P, 1024], BF16, name="xw0")
            for j in range(2):
                nc.tensor.matmul(
                    out=xw0[:, j * 512 : (j + 1) * 512],
                    lhsT=ident_bf[:],
                    rhs=xp[:, j * XL + c * XWIN : j * XL + c * XWIN + 512],
                    start=True,
                    stop=True,
                )
            xw_of[c] = xw0
            if c < NCH - 1:
                return
            nc.tensor.matmul(
                out=xw2,
                lhsT=ident_bf[:],
                rhs=xp[:, 2 * XL + c * XWIN : 2 * XL + c * XWIN + 512],
                start=True,
                stop=True,
            )

        def stage_pass(u):
            c, taps = units[u]
            ps_of[u] = []
            for k0 in range(0, len(taps), 2):
                ps = psum.tile([P, 512], F32, tag="mm", name="ps")
                for k, t in enumerate(taps[k0 : k0 + 2]) if k0 + 1 < len(taps) else [(0, taps[k0])] * 2:
                    nc.tensor.matmul_mx(
                        out=ps[:, k * CHQ : (k + 1) * CHQ],
                        lhsT=ws_codes[:, t * P : (t + 1) * P].bitcast(FP8X4),
                        lhsT_scale=ws_scl[:, t * P : (t + 1) * P],
                        rhs=red_codes[:, c * CHQ : (c + 1) * CHQ].bitcast(FP8X4),
                        rhs_scale=red_scl[:, c * CHQ : (c + 1) * CHQ],
                        start=True,
                        stop=True,
                    )
                ps_of[u].append(ps)

        def stage_max(u, k):
            c, taps = units[u]
            if k >= len(taps):
                return
            t = taps[k]
            if t == 0:
                mm_of[c] = stage.tile([P, 512], F32, name="mm", bufs=2)
            mk = mm_of[c][:, k % 2 * CHQ : (k % 2 + 1) * CHQ]
            pk = ps_of[u][k // 2][:, k % 2 * CHQ : (k % 2 + 1) * CHQ]
            if t < 2:
                nc.vector.tensor_scalar_add(out=mk, in0=pk, scalar1=bs[:, t : t + 1])
            else:
                nc.vector.scalar_tensor_tensor(
                    out=mk, in0=pk, scalar=bs[:, t : t + 1], in1=mk, op0=ALU.add, op1=ALU.max
                )

        def stage_copy(u, b):
            n = min(2, len(units[u][1]) - 2 * b) * CHQ
            if b == 0:
                kb_of[u] = stage.tile([P, 4 * CHQ], F32, name="kb", bufs=LEAD + 1)
            nc.scalar.copy(out=kb_of[u][:, 2 * b * CHQ : 2 * b * CHQ + n], in_=ps_of[u][b][:, 0:n])

        def merge_max(c):
            ms = stage.tile([P, CHQ], F32, name="ms", bufs=2)
            nc.vector.tensor_tensor(out=ms[:], in0=mm_of[c][:, 0:CHQ], in1=mm_of[c][:, CHQ : 2 * CHQ], op=ALU.max)
            ms_of[c] = ms

        def max_to_psum(c):
            nc.tensor.matmul(out=mp, lhsT=ident[:], rhs=ms_of[c][:], start=True, stop=True)

        def stage_sub(u):
            c, taps = units[u]
            n = len(taps)
            kb3 = kb_of[u][:, 0 : n * CHQ].rearrange("p (k q) -> p k q", k=n)
            nc.vector.tensor_tensor(
                out=kb3,
                in0=kb3,
                in1=mp.unsqueeze(1).to_broadcast([P, n, CHQ]),
                op=ALU.subtract,
            )

        def stage_exp(u):
            c, taps = units[u]
            e = main.tile([P, 4 * CHQ], F32, name="e", bufs=4)
            for k, t in enumerate(taps):
                nc.scalar.activation(
                    out=e[:, k * CHQ : (k + 1) * CHQ],
                    in_=kb_of[u][:, k * CHQ : (k + 1) * CHQ],
                    func=ACT.Exp,
                    bias=bs[:, t : t + 1],
                    scale=1.0,
                )
            e_of[u] = e

        def vector_has_channel_2(u):
            return u >= n_units - upc and u % upc in (4, 6, 8, 10)

        def product_gpsimd(u):
            c, taps = units[u]
            n = len(taps)
            j0 = 1 if vector_has_channel_2(u) else 0
            ng = 2 - j0
            pg = main.tile([P, 8 * CHQ], F32, name="pg", bufs=3)
            s0 = taps[0] % K7
            q0 = (taps[0] // K7 + c * CHR) * W
            nc.gpsimd.tensor_tensor(
                out=pg[:, 0 : n * ng * CHQ].rearrange("p (k j q) -> p k j q", k=n, j=ng),
                in0=e_of[u][:, 0 : n * CHQ]
                .rearrange("p (k q) -> p k q", k=n)
                .unsqueeze(2)
                .to_broadcast([P, n, ng, CHQ]),
                in1=xs[:].rearrange("p (s j q) -> p s j q", s=K7, j=2)[:, s0 : s0 + n, j0:2, q0 : q0 + CHQ],
                op=ALU.mult,
            )
            pr_of[u] = [[pg[:, (k * ng * QB + i) * P : (k * ng * QB + i + 1) * P] for i in range(ng * QB)] for k in range(n)]
            nv_of[u] = 4 - ng

        def product_vector(u, k):
            c, taps = units[u]
            if k >= len(taps):
                return
            off = (taps[k] // K7) * XK + taps[k] % K7
            ek3 = e_of[u][:, k * CHQ : (k + 1) * CHQ].rearrange("p (h w) -> p h w", w=W)
            pv = main.tile([P, 2 * CHQ], F32, name="pv", bufs=10)
            nc.vector.tensor_tensor(
                out=pv[:].rearrange("p (j h w) -> p j h w", j=2, w=W),
                in0=xw_of[c][:]
                .rearrange("p (j n) -> p j n", j=2)[:, :, off : off + XWIN]
                .rearrange("p j (h k) -> p j h k", k=XK)[:, :, :, 0:W],
                in1=ek3.unsqueeze(1).to_broadcast([P, 2, CHR, W]),
                op=ALU.mult,
            )
            blocks = [pv[:, i * P : (i + 1) * P] for i in range(2 * QB)]
            if vector_has_channel_2(u):
                pv2 = main.tile([P, CHQ], F32, tag="pv", name="pv2", bufs=10)
                nc.vector.tensor_tensor(
                    out=pv2[:].rearrange("p (h w) -> p h w", w=W),
                    in0=xw2[:, off : off + XWIN].rearrange("p (h k) -> p h k", k=XK)[:, :, 0:W],
                    in1=ek3,
                    op=ALU.mult,
                )
                blocks += [pv2[:, i * P : (i + 1) * P] for i in range(QB)]
            pr_of[u][k] = blocks + pr_of[u][k]

        def add_block(bank, slot, block, first, last, as_matmul=False):
            if as_matmul:
                nc.tensor.matmul(
                    out=bank[:, slot * P : (slot + 1) * P], lhsT=block, rhs=ident[:], start=first, stop=last
                )
            else:
                nc.tensor.matmul(
                    out=bank[:, slot * P : (slot + 1) * P],
                    lhsT=block,
                    rhs=ident[:],
                    start=first,
                    stop=last,
                    is_transpose=True,
                )

        def add_z(u, k):
            c, taps = units[u]
            if k >= len(taps):
                return
            t = taps[k]
            if t == 0:
                z_of[c] = pacc.tile([P, 512], F32, tag="acc0", name="acc")
            for qb in range(QB):
                q0 = k * CHQ + qb * P
                add_block(
                    z_of[c], qb, e_of[u][:, q0 : q0 + P], t == 0 and qb == 0, t == KK - 1 and qb == QB - 1
                )

        def add_tap(u, k, of_vector):
            c, taps = units[u]
            if k >= len(taps):
                return
            t = taps[k]
            first = t == 0
            last = t == KK - 1
            if first:
                acc_of.setdefault(c, [])
                acc_of[c].append(pacc.tile([P, 512], F32, tag="acc%d" % (1 if of_vector else 2), name="acc"))
            n_vector = nv_of[u] * QB
            for i in range(n_vector) if of_vector else range(n_vector, CC * QB):
                slot = i % (2 * QB)
                add_block(
                    acc_of[c][i // (2 * QB)],
                    slot,
                    pr_of[u][k][i],
                    first and slot == 0,
                    last and slot == 2 * QB - 1,
                    as_matmul=of_vector and k == 0 and i in (2, 3),
                )

        def empty_z(c):
            zs = main.tile([P, CHQ], F32, name="zs", bufs=1)
            nc.scalar.copy(out=zs[:], in_=z_of[c][:, 0:CHQ])
            return zs

        def empty_a(c):
            sums = const.tile([P, 1024], F32, tag="xh1", name="sums")
            nc.scalar.copy(out=sums[:, 0:512], in_=acc_of[c][0][:])
            return sums

        def empty_b(c, sums):
            nc.scalar.copy(out=sums[:, 512:1024], in_=acc_of[c][1][:])

        def turn_back(block):
            tb = psum.tile([P, 512], F32, tag="mm", name="tb")
            for s in range(block.shape[1] // P):
                nc.tensor.transpose(tb[:, s * P : (s + 1) * P], block[:, s * P : (s + 1) * P], ident[:])
            return tb

        def reciprocal_z(tb):
            rz = main.tile([P, CHQ], F32, name="rz", bufs=1)
            nc.vector.reciprocal(out=rz[:], in_=tb[:, 0:CHQ])
            return rz

        def scale_pair(c, i, tb, rz):
            if i == 0:
                osb_of[c] = const.tile([P, CC * CHQ], F32, tag="xh0", name="osb")
            osb = osb_of[c]
            nc.vector.tensor_tensor(
                out=osb[:, i * 512 : (i + 1) * 512].rearrange("p (j n) -> p j n", j=2),
                in0=tb[:].rearrange("p (j n) -> p j n", j=2),
                in1=rz[:].unsqueeze(1).to_broadcast([P, 2, CHQ]),
                op=ALU.mult,
            )
            nc.sync.dma_start(
                out=out_v[:, 2 * i : 2 * i + 2, c * CHQ : (c + 1) * CHQ],
                in_=osb[:, i * 512 : (i + 1) * 512].rearrange("p (j q) -> p j q", j=2),
            )

        def stage_kern(u):
            stage_pass(u)
            for b in range(2):
                stage_max(u, 2 * b)
                stage_max(u, 2 * b + 1)
                stage_copy(u, b)

        with tc.tile_pool(name="head", bufs=1) as head:
            ident = const.tile([P, P], F32)
            make_identity(nc, ident[:])
            ident_bf = const.tile([P, P], BF16)
            make_identity(nc, ident_bf[:])

            wr_sb = head.tile([P, 4 * 512], BF16)
            x_half = [const.tile([P, CC * 512], BF16, tag="xh%d" % i, name="xh") for i in range(2)]
            br_b = const.tile([P, 4], BF16)
            bs_b = const.tile([P, KK], BF16)
            br = const.tile([P, 4], F32)
            bs = const.tile([P, KK], F32)
            xp = const.tile([P, 3 * XL], BF16)
            xs = const.tile([P, K7 * 2 * XROWS], BF16)
            xs5 = xs[:].rearrange("p (s j h w) -> p s j h w", s=K7, j=2, w=W)
            gw = head.tile([P, 4 * P * 4], BF16, align_bytes=64)
            wr_codes = const.tile([P, 4 * P], U32, align_bytes=64)
            wr_scl = const.tile([P, 4 * P], U8, align_bytes=64)
            x_codes = const.tile([P, HW], U32, align_bytes=64)
            x_scl = const.tile([P, HW], U8, align_bytes=64)
            red_codes = const.tile([P, HW], U32, align_bytes=64)
            red_scl = const.tile([P, HW], U8, align_bytes=64)
            ws_codes = const.tile([P, KK * P], U32, align_bytes=64)
            ws_scl = const.tile([P, KK * P], U8, align_bytes=64)
            groups = {}
            red_of = {}
            ws_tiles = []
            gws_of = {}
            x_view = x[0].rearrange("(g j) h w -> g j (h w)", j=CC)
            ws_view = w_span.rearrange("(g t) r -> g t r", t=KK)

            def load_x(i, q0, q1):
                nc.sync.dma_start(
                    out=x_half[i][:].rearrange("p (j q) -> p j q", j=CC)[:, :, q0:q1],
                    in_=x_view[:, :, i * 512 + q0 : i * 512 + q1],
                )

            def load_ws(a):
                n = min(WS_TAPS, KK - a * WS_TAPS)
                ws_sb = head.tile([P, WS_TAPS * R], BF16, name="ws_sb", bufs=4)
                nc.sync.dma_start(
                    out=ws_sb[:, 0 : n * R].rearrange("p (t r) -> p t r", t=n),
                    in_=ws_view[:, a * WS_TAPS : a * WS_TAPS + n, :],
                )
                ws_tiles.append(ws_sb)

            def fill_xp(i):
                x0 = PAD + (PAD + i * H // 2) * XK
                nc.gpsimd.tensor_scalar(
                    out=xp[:]
                    .rearrange("p (j n) -> p j n", j=3)[:, :, x0 : x0 + H // 2 * XK]
                    .rearrange("p j (h k) -> p j h k", k=XK)[:, :, :, 0:W],
                    in0=x_half[i][:].rearrange("p (j h w) -> p j h w", j=CC, w=W)[:, 0:3, :, :],
                    scalar1=1.0,
                    scalar2=0.0,
                    op0=ALU.mult,
                    op1=ALU.add,
                )

            def zero_xs_rows():
                for rows in (slice(0, PAD), slice(HP - PAD, HP)):
                    nc.gpsimd.memset(
                        xs[:].rearrange("p (n h w) -> p n (h w)", h=HP, w=W)[:, :, rows.start * W : rows.stop * W], 0.0
                    )

            def zero_xs_columns():
                for s in range(K7):
                    d = s - PAD
                    if d != 0:
                        cols = slice(0, 4) if d < 0 else slice(W - 4, W)
                        nc.vector.memset(xs5[:, s, :, PAD : HP - PAD, cols], 0.0)

            def xs_views(s, h0, h1):
                i = h0 // (H // 2)
                d = s - PAD
                w0, w1 = max(0, -d), min(W, W - d)
                r0 = h0 + PAD
                src = x_half[i][:].rearrange("p (j h w) -> p j h w", j=CC, w=W)
                b = i * (H // 2)
                return xs5[:, s, :, r0 : r0 + h1 - h0, w0:w1], src[:, 2:4, h0 - b : h1 - b, w0 + d : w1 + d]

            def fill_xs_gpsimd(s, h0, h1):
                dst, src = xs_views(s, h0, h1)
                nc.gpsimd.tensor_scalar(out=dst, in0=src, scalar1=1.0, scalar2=0.0, op0=ALU.mult, op1=ALU.add)

            def fill_xs_scalar(s, h0, h1):
                dst, src = xs_views(s, h0, h1)
                nc.scalar.copy(out=dst, in_=src)

            def turn_wr(b):
                wr32 = wr_sb[:].bitcast(F32).rearrange("p (a w v) -> p a v w", a=4, v=2)
                gw32 = gw[:].bitcast(F32).rearrange("p (a r v) -> p a r v", a=4, v=2)
                tp = pacc.tile([P, 512], F32, tag="acc%d" % b, name="tp")
                for a2 in range(2):
                    for v in range(2):
                        nc.tensor.transpose(
                            tp[:, (a2 * 2 + v) * P : (a2 * 2 + v + 1) * P], wr32[:, 2 * b + a2, v, :], ident[:]
                        )
                nc.scalar.copy(
                    out=gw32[:, 2 * b : 2 * b + 2, :, :], in_=tp[:].rearrange("p (a v r) -> p a r v", a=2, v=2)
                )

            def group(key, src, engine_copy):
                groups[key] = const.tile([P, 4 * CHQ], BF16, tag="grp", name="grp", bufs=2, align_bytes=64)
                engine_copy(
                    out=groups[key][:].rearrange("p (q j) -> p q j", j=4), in_=src.rearrange("p j q -> p q j")
                )

            def group_x(c, engine_copy):
                q0 = c % 2 * CHQ
                group(("x", c), x_half[c // 2][:].rearrange("p (j q) -> p j q", j=CC)[:, :, q0 : q0 + CHQ], engine_copy)

            def group_red(c, engine_copy):
                group(("red", c), red_of[c][:].rearrange("p (a q) -> p a q", a=4), engine_copy)

            def quantise_chunk(codes, scl, c, key):
                nc.vector.quantize_mx(
                    out=codes[:, c * CHQ : (c + 1) * CHQ].bitcast(FP8X4),
                    scales=scl[:, c * CHQ : (c + 1) * CHQ],
                    in_=groups[key, c][:],
                )

            def red_passes(c, a0, shared):
                if a0 == 0:
                    red_of[c] = const.tile([P, 4 * CHQ], BF16, tag="red", name="red", bufs=2)
                ps = psum.tile([P, 512], F32, tag="mm", name="ps")
                for i in range(2):
                    a = a0 + i
                    nc.tensor.matmul_mx(
                        out=ps[:, i * CHQ : (i + 1) * CHQ],
                        lhsT=wr_codes[:, a * P : (a + 1) * P].bitcast(FP8X4),
                        lhsT_scale=wr_scl[:, a * P : (a + 1) * P],
                        rhs=x_codes[:, c * CHQ : (c + 1) * CHQ].bitcast(FP8X4),
                        rhs_scale=x_scl[:, c * CHQ : (c + 1) * CHQ],
                        start=True,
                        stop=True,
                    )
                for i in range(2):
                    a = a0 + i
                    dst = red_of[c][:, a * CHQ : (a + 1) * CHQ]
                    src = ps[:, i * CHQ : (i + 1) * CHQ]
                    if shared and a0 == 2:
                        nc.vector.tensor_scalar(
                            out=dst, in0=src, scalar1=br[:, a : a + 1], scalar2=0.0, op0=ALU.add, op1=ALU.max
                        )
                    else:
                        nc.scalar.activation(out=dst, in_=src, func=ACT.Relu, bias=br[:, a : a + 1], scale=1.0)

            n_groups = (KK + 3) // 4

            def turn_ws(g):
                n = min(4, KK - 4 * g)
                ws32 = ws_tiles[4 * g // WS_TAPS][:].bitcast(F32).rearrange("p (t u w) -> p t u w", t=WS_TAPS, u=2)
                gws = head.tile([P, 4 * P * 4], BF16, name="gws", bufs=3, align_bytes=64)
                gws32 = gws[:].bitcast(F32).rearrange("p (t g u) -> p t g u", t=4, u=2)
                for b in range((n + 1) // 2):
                    nb = min(2, n - 2 * b)
                    tp = pacc.tile([P, 512], F32, tag="acc%d" % ((2 * g + b) % 3), name="tp")
                    for tl in range(nb):
                        for u in range(2):
                            nc.tensor.transpose(
                                tp[:, (tl * 2 + u) * P : (tl * 2 + u + 1) * P],
                                ws32[:, 4 * g % WS_TAPS + 2 * b + tl, u, :],
                                ident[:],
                            )
                    copy = nc.vector.tensor_copy if b == 1 and g % 6 == 5 else nc.scalar.copy
                    copy(
                        out=gws32[:, 2 * b : 2 * b + nb, :, :],
                        in_=tp[:].rearrange("p (t u g) -> p t g u", t=2, u=2)[:, 0:nb, :, :],
                    )
                gws_of[g] = gws
                if (4 * g + 4) % WS_TAPS == 0 and (len(ws_tiles)) * WS_TAPS < KK:
                    load_ws(len(ws_tiles))

            def quantise_ws(g):
                n = min(4, KK - 4 * g)
                nc.vector.quantize_mx(
                    out=ws_codes[:, 4 * g * P : (4 * g + n) * P].bitcast(FP8X4),
                    scales=ws_scl[:, 4 * g * P : (4 * g + n) * P],
                    in_=gws_of[g][:, 0 : n * P * 4],
                )

            with tc.manual_schedule():
                nc.sync.dma_start(
                    out=wr_sb[:].rearrange("p (u f) -> p u f", u=2),
                    in_=w_reduce.rearrange("(u p e) c -> p u (e c)", u=2, e=2),
                )
                load_x(0, 0, CHQ)
                with nc.allow_non_contiguous_dma(reason="two small bias vectors"):
                    nc.sync.dma_start(
                        out=br_b[:].rearrange("p (u e) -> p u e", u=2),
                        in_=b_reduce.rearrange("(u p e) -> p u e", u=2, e=2),
                    )
                    load_ws(0)
                    nc.sync.dma_start(out=bs_b[:], in_=b_span.rearrange("(g t) -> g t", t=KK))
                load_x(0, CHQ, 512)
                load_ws(1)
                load_x(1, 0, 512)
                load_ws(2)
                load_ws(3)

                nc.gpsimd.memset(xp[:].bitcast(F32), 0.0)
                zero_xs_rows()
                zero_xs_columns()
                nc.vector.memset(br[:], 0.0)
                warm = const.tile([P, 1], F32)
                nc.scalar.activation(out=warm[:], in_=br[:, 0:1], func=ACT.Exp, scale=1.0)
                fill_xp(0)
                fill_xp(1)
                for s in range(K7):
                    fill_xs_gpsimd(s, 0, CHR + PAD)

                turn_wr(0)
                turn_wr(1)
                group_x(0, nc.vector.tensor_copy)
                nc.vector.tensor_copy(out=br[:], in_=br_b[:])
                nc.vector.quantize_mx(out=wr_codes[:].bitcast(FP8X4), scales=wr_scl[:], in_=gw[:])
                quantise_chunk(x_codes, x_scl, 0, "x")
                red_passes(0, 0, True)
                red_passes(0, 2, True)
                turn_ws(0)
                nc.vector.tensor_copy(out=bs[:], in_=bs_b[:])
                group_red(0, nc.vector.tensor_copy)
                turn_ws(1)
                quantise_ws(0)
                quantise_chunk(red_codes, red_scl, 0, "red")
                done = 0
                for g in range(1, n_groups + 2):
                    if g + 1 < n_groups:
                        turn_ws(g + 1)
                    if g < n_groups:
                        quantise_ws(g)
                    while done < upc and units[done][1][-1] < 4 * g:
                        stage_kern(done)
                        done += 1
                    if g == 4:
                        load_windows(0)
                    if g == 5:
                        group_x(1, nc.vector.tensor_copy)
                        quantise_chunk(x_codes, x_scl, 1, "x")
                    if g in (6, 7):
                        red_passes(1, 2 * g - 12, False)
                    if g == 9:
                        group_red(1, nc.vector.tensor_copy)
                        quantise_chunk(red_codes, red_scl, 1, "red")
                merge_max(0)

            late_steps = []
            for c in (2, 3):
                late_steps += [
                    [lambda c=c: group_x(c, nc.scalar.copy)],
                    [lambda c=c: quantise_chunk(x_codes, x_scl, c, "x"), lambda c=c: red_passes(c, 0, False)],
                    [lambda c=c: red_passes(c, 2, False)],
                    [lambda c=c: group_red(c, nc.scalar.copy)],
                    [lambda c=c: quantise_chunk(red_codes, red_scl, c, "red")],
                ]
            late_steps += [
                [lambda s=s, h=h: fill_xs_scalar(s, *h) for s in ss for h in ((CHR + PAD, H // 2), (H // 2, H))]
                for ss in ((0, 1), (2, 3), (4, 5), (6,))
            ]
        main = ctx.enter_context(tc.tile_pool(name="main", bufs=1))

        with tc.manual_schedule():
            max_to_psum(0)
            stage_sub(0)
            stage_exp(0)
            stage_sub(1)
            for u in range(upc, LEAD):
                stage_kern(u)
            stage_pass(LEAD)
            for n in range(n_units):
                c, taps = units[n]
                last_k = len(taps) - 1
                ends = n % upc == upc - 1
                back = n % upc if c > 0 else upc
                ahead = n + LEAD < n_units
                if back == 1:
                    tb = turn_back(zs)
                elif back in (2, 3):
                    tb = turn_back(sums[:, (back - 2) * 512 : (back - 1) * 512])
                if n + 1 < n_units:
                    stage_exp(n + 1)
                if back == 0:
                    zs = empty_z(c - 1)
                    sums = empty_a(c - 1)
                elif back == 1:
                    empty_b(c - 1, sums)
                product_gpsimd(n)
                if n == n_units - 1:
                    for k in range(4):
                        add_z(n, k)
                    zs = empty_z(c)
                    tb = turn_back(zs)
                for k in range(4):
                    product_vector(n, k)
                    if k == 0 and n + 2 < n_units:
                        stage_sub(n + 2)
                    if ahead and k == 1:
                        stage_max(n + LEAD, 0)
                        stage_max(n + LEAD, 1)
                        stage_copy(n + LEAD, 0)
                    if ahead and k == 2:
                        stage_max(n + LEAD, 2)
                    if ahead and k == 3:
                        stage_max(n + LEAD, 3)
                        stage_copy(n + LEAD, 1)
                    if k == last_k and ends and c + 1 < NCH:
                        load_windows(c + 1)
                    if n < n_units - 1:
                        add_z(n, k)
                    add_tap(n, k, True)
                if back == 1:
                    rz = reciprocal_z(tb)
                elif back in (2, 3):
                    scale_pair(c - 1, back - 2, tb, rz)
                if n + LEAD + 1 < n_units:
                    stage_pass(n + LEAD + 1)
                if ahead and (n + LEAD) % upc == upc - 1:
                    merge_max((n + LEAD) // upc)
                    max_to_psum((n + LEAD) // upc)
                if n > 0:
                    for k in range(4):
                        add_tap(n - 1, k, False)
                if n < len(late_steps):
                    for step in late_steps[n]:
                        step()
            rz = reciprocal_z(tb)
            sums = empty_a(NCH - 1)
            for k in range(4):
                add_tap(n_units - 1, k, False)
            scale_pair(NCH - 1, 0, turn_back(sums[:, 0:512]), rz)
            empty_b(NCH - 1, sums)
            scale_pair(NCH - 1, 1, turn_back(sums[:, 512:1024]), rz)
